import numpy as np
import ml_dtypes


def mxq(x, axis, fmt="e4m3"):
    dtype, down = {"e4m3": (ml_dtypes.float8_e4m3fn, 7), "e5m2": (ml_dtypes.float8_e5m2, 14)}[fmt]
    v = np.moveaxis(np.asarray(x, np.float32).astype(ml_dtypes.bfloat16).astype(np.float64), axis, -1)
    blocks = v.reshape(v.shape[:-1] + (-1, 32))
    amax = np.abs(blocks).max(-1, keepdims=True)
    byte = np.maximum(np.where(amax > 0, np.frexp(amax)[1] - 1 + 127, 0) - down, 1)
    scale = np.exp2(byte - 127.0)
    codes = (blocks / scale).astype(np.float32).astype(dtype).astype(np.float64)
    return np.moveaxis((codes * scale).reshape(v.shape), -1, axis)


WIDE = False


def mx_kscale(k):
    if not WIDE:
        return np.ones(k)
    levels = np.array([10, -10, 5, -5, 0])
    a = np.random.permutation(np.resize(levels, k // 512 * 4)).reshape(k // 512, 4)
    idx = np.arange(k)
    return np.exp2(a[idx // 512, idx % 128 // 32])


BF16 = ml_dtypes.bfloat16


def bf(x):
    return np.asarray(x, np.float32).astype(BF16)


def f64(x):
    return np.asarray(x).astype(np.float64)


E2M1 = np.array([0.0, 0.5, 1.0, 1.5, 2.0, 3.0, 4.0, 6.0, -0.0, -0.5, -1.0, -1.5, -2.0, -3.0, -4.0, -6.0])


def pack_weight(w, fmt):
    k, n = w.shape
    w = f64(bf(w)).reshape(k // 32, 32, n)
    amax = np.abs(w).max(1)
    if fmt == "e4m3":
        byte = np.frexp(amax)[1] - 1 + 127 - 7
    else:
        mant, ex = np.frexp(amax / 6.0)
        byte = np.where(mant > 0.5, ex, ex - 1) + 127
    byte = np.clip(np.where(amax > 0, byte, 1), 1, 254)
    scaled = (w * np.exp2(127.0 - byte)[:, None, :]).reshape(k, n).astype(np.float32)
    by_word = np.ascontiguousarray(scaled.reshape(k // 512, 128, 4, n).transpose(0, 1, 3, 2))
    if fmt == "e4m3":
        words = by_word.astype(ml_dtypes.float8_e4m3fn).view(np.uint8)
    else:
        c = by_word.astype(ml_dtypes.float4_e2m1fn).view(np.uint8) & 0xF
        words = c[..., 0::2] | (c[..., 1::2] << 4)
    return np.ascontiguousarray(words), np.ascontiguousarray(byte.astype(np.uint8).reshape(k // 512, 16, n))


def unpack_weight(words, scales, fmt):
    g, p, n, _ = words.shape
    if fmt == "e4m3":
        vals = np.ascontiguousarray(words).view(ml_dtypes.float8_e4m3fn).astype(np.float64)
    else:
        nib = np.empty((g, p, n, 4), np.uint8)
        nib[..., 0::2] = words & 0xF
        nib[..., 1::2] = words >> 4
        vals = E2M1[nib]
    vals = vals * np.repeat(np.exp2(scales.astype(np.float64) - 127.0), 8, axis=1)[..., None]
    return vals.transpose(0, 1, 3, 2).reshape(g * 512, n)


B, NV, NH, NT = 4096, 2048, 512, 2
FMT = "e4m3"


def softplus(v):
    return np.logaddexp(v, 0.0)


def softmax_last(v):
    e = np.exp(v - v.max(axis=1, keepdims=True))
    return e / e.sum(axis=1, keepdims=True)


def setup_inputs():
    s = mx_kscale(NV)
    input_data = bf(np.random.standard_normal((B, NV)) * s)
    w = np.random.standard_normal((NH, NV)) / np.sqrt(NV) / s[None, :]
    words, scales = pack_weight(np.ascontiguousarray(w.T), FMT)
    return {"input_data": input_data,
            "W_words": words,
            "W_scales": scales,
            "U": bf(np.random.standard_normal((NH, NT)) * 0.5),
            "h_bias": bf(np.random.standard_normal((1, NH)) * 0.5 - np.log(NH / 16.0)),
            "y_bias": bf(np.random.standard_normal((1, NT)) * 0.5)}


def reference(input_data, W_words, W_scales, U, h_bias, y_bias):
    pf = (mxq(f64(input_data), 1, "e4m3") @ unpack_weight(W_words, W_scales, FMT)) + f64(h_bias)
    sp = softplus(pf[:, :, None] + f64(U)[None, :, :])
    logits = f64(y_bias) + sp.sum(axis=1)
    return softmax_last(logits)

@@ -1,0 +1,220 @@
+from contextlib import ExitStack
+
+import concourse.mybir as mybir
+from concourse.masks import make_identity
+
+F32 = mybir.dt.float32
+BF16 = mybir.dt.bfloat16
+I32 = mybir.dt.int32
+U32 = mybir.dt.uint32
+U8 = mybir.dt.uint8
+FP8X4 = mybir.dt.float8_e4m3fn_x4
+ACT = mybir.ActivationFunctionType
+ALU = mybir.AluOpType
+
+P = 128
+BATCH, VISIBLE, HIDDEN = 4096, 2048, 512
+K_PASS = 4 * P
+PASSES = VISIBLE // K_PASS
+WORDS = K_PASS // 2
+HID_TILES = HIDDEN // P
+BATCH_TILES = BATCH // P
+CHUNK_TILES = 4
+CHUNK = CHUNK_TILES * P
+CHUNKS = BATCH_TILES // CHUNK_TILES
+X_AHEAD = 3
+
+FLOPS = 2 * BATCH * VISIBLE * HIDDEN
+
+
+def tile_rbm_kernel(tc, input_data, W_words, W_scales, U, h_bias, y_bias, out):
+    nc = tc.nc
+    x_by_tile = input_data.rearrange("(p i) k -> i p k", i=BATCH_TILES)
+
+    with ExitStack() as stack:
+        const = stack.enter_context(tc.tile_pool(name="const", bufs=1))
+        x_pool = stack.enter_context(tc.tile_pool(name="x", bufs=X_AHEAD * CHUNK_TILES))
+        mx_pool = stack.enter_context(tc.tile_pool(name="mx", bufs=2))
+        on_pool = stack.enter_context(tc.tile_pool(name="on", bufs=2 * HID_TILES))
+        arg_pool = stack.enter_context(tc.tile_pool(name="arg", bufs=2))
+        flip_pool = stack.enter_context(tc.psum_pool(name="flip", bufs=4))
+        acc_pool = stack.enter_context(tc.psum_pool(name="acc", bufs=3))
+        stack.enter_context(tc.manual_schedule())
+
+        w_planes = const.tile([P, PASSES, HIDDEN], U8, align_bytes=64)
+        nc.vector.memset(w_planes[:].bitcast(I32), 0)
+        for quad in range(4):
+            nc.sync.dma_start(
+                out=w_planes[32 * quad : 32 * quad + 4, :, :].bitcast(I32),
+                in_=W_scales[:, 4 * quad : 4 * quad + 4, :].rearrange("g r n -> r g n").bitcast(I32),
+            )
+
+        h_rows = const.tile([HID_TILES, P], BF16)
+        u_rows = const.tile([HID_TILES, P, 2], BF16)
+        y_all = const.tile([P, 2], BF16)
+        nc.scalar.dma_start(out=h_rows[:], in_=h_bias.rearrange("o (t p) -> (o t) p", p=P))
+        nc.scalar.dma_start(out=u_rows[:], in_=U.rearrange("(t p) c -> t p c", p=P))
+        nc.scalar.dma_start(out=y_all[:], in_=y_bias.rearrange("o c -> (o c)").partition_broadcast(P))
+
+        ident = const.tile([P, P], F32)
+        make_identity(nc, ident[:])
+
+        x_tiles = {}
+
+        def load_x(i):
+            x_tiles[i] = x_pool.tile([P, VISIBLE], BF16, name="x_tile")
+            nc.sync.dma_start(out=x_tiles[i][:], in_=x_by_tile[i])
+
+        w_codes = const.tile([P, PASSES, HIDDEN], U32, align_bytes=64)
+        for i in range(6):
+            load_x(i)
+        nc.sync.dma_start(
+            out=w_codes[:].bitcast(I32),
+            in_=W_words.rearrange("g p n t -> p g (n t)").bitcast(I32),
+        )
+        for i in range(6, X_AHEAD * CHUNK_TILES):
+            load_x(i)
+
+        as_rows = const.tile([P, 3, P], F32)
+        nc.vector.memset(as_rows[:], 0.0)
+        nc.vector.tensor_copy(out=as_rows[0:HID_TILES, 0, :], in_=h_rows[:])
+        nc.vector.tensor_copy(out=as_rows[0:HID_TILES, 1:3, :], in_=u_rows[:].rearrange("t p c -> t c p"))
+        as_cols_ps = acc_pool.tile([P, 3, P], F32, name="acc")
+        for m in range(3):
+            nc.tensor.transpose(as_cols_ps[:, m, :], as_rows[:, m, :], ident[:])
+        as_cols = const.tile([P, 3, HID_TILES], F32)
+        nc.vector.tensor_copy(out=as_cols[:], in_=as_cols_ps[:, :, 0:HID_TILES])
+        sig_bias = const.tile([P, HID_TILES], F32)
+        u_diff = const.tile([P, HID_TILES], F32)
+        nc.vector.tensor_add(out=sig_bias[:], in0=as_cols[:, 0, :], in1=as_cols[:, 2, :])
+        nc.vector.tensor_sub(out=u_diff[:], in0=as_cols[:, 1, :], in1=as_cols[:, 2, :])
+        sig_pos = const.tile([P, HID_TILES], F32)
+        sig_neg = const.tile([P, HID_TILES], F32)
+        nc.scalar.activation(out=sig_pos[:], in_=u_diff[:], func=ACT.Sigmoid)
+        nc.scalar.activation(out=sig_neg[:], in_=u_diff[:], func=ACT.Sigmoid, scale=-1.0)
+        inv_neg = const.tile([P, HID_TILES], F32)
+        ratio = const.tile([P, HID_TILES], F32)
+        gain = const.tile([P, HID_TILES], F32)
+        nc.vector.reciprocal(out=inv_neg[:], in_=sig_neg[:])
+        nc.vector.tensor_mul(out=ratio[:], in0=sig_pos[:], in1=inv_neg[:])
+        nc.vector.tensor_scalar_add(out=gain[:], in0=ratio[:], scalar1=-1.0)
+        y_diff = const.tile([P, 1], F32)
+        y_diff_neg = const.tile([P, 1], F32)
+        nc.vector.tensor_sub(out=y_diff[:], in0=y_all[:, 0:1], in1=y_all[:, 1:2])
+        nc.vector.tensor_sub(out=y_diff_neg[:], in0=y_all[:, 1:2], in1=y_all[:, 0:1])
+
+        grouped = {}
+        codes = {}
+        planes = {}
+        on = {}
+        half_product = {}
+        product = const.tile([P, CHUNKS, CHUNK], F32)
+
+        def transpose_x(i):
+            c, j = divmod(i, CHUNK_TILES)
+            if j == 0:
+                grouped[c] = mx_pool.tile([P, PASSES, 4 * CHUNK], BF16, name="grouped", align_bytes=64)
+            x_words = x_tiles[i][:].bitcast(F32)
+            dest = grouped[c][:].bitcast(F32).rearrange("p g (b u) -> p g b u", u=2)
+            for half in range(2):
+                bank = flip_pool.tile([P, 2, 2, P], F32, name="bank")
+                for gg in range(2):
+                    first = WORDS * (2 * half + gg)
+                    for u in range(2):
+                        nc.tensor.transpose(bank[:, gg, u, :], x_words[:, first + u : first + WORDS : 2], ident[:])
+                copy_out = nc.vector.tensor_copy if (2 * i + half) % 4 == 3 else nc.scalar.copy
+                copy_out(
+                    out=dest[:, 2 * half : 2 * half + 2, j * P : (j + 1) * P, :],
+                    in_=bank[:].rearrange("p g u b -> p g b u"),
+                )
+
+        def quantise(c):
+            codes[c] = mx_pool.tile([P, PASSES, CHUNK], U32, name="codes", align_bytes=64)
+            planes[c] = mx_pool.tile([P, PASSES, CHUNK], U8, name="planes", align_bytes=64)
+            for g in range(PASSES):
+                nc.vector.quantize_mx(
+                    out=codes[c][:, g, :].bitcast(FP8X4),
+                    scales=planes[c][:, g, :],
+                    in_=grouped[c][:, g, :],
+                )
+
+        def multiply(c, t):
+            hid = slice(t * P, (t + 1) * P)
+            acc = acc_pool.tile([P, CHUNK], F32, name="acc")
+            for g in range(PASSES):
+                nc.tensor.matmul_mx(
+                    out=acc[:],
+                    lhsT=w_codes[:, g, hid].bitcast(FP8X4),
+                    lhsT_scale=w_planes[:, g, hid],
+                    rhs=codes[c][:, g, :].bitcast(FP8X4),
+                    rhs_scale=planes[c][:, g, :],
+                    start=(g == 0),
+                    stop=(g == PASSES - 1),
+                )
+            on[(c, t)] = on_pool.tile([P, CHUNK], F32, name="on")
+            nc.scalar.activation(out=on[(c, t)][:], in_=acc[:], func=ACT.Sigmoid, bias=sig_bias[:, t : t + 1])
+
+        def multiply_arguments(c, t, result):
+            arg_a = arg_pool.tile([P, CHUNK], F32, name="arg_a")
+            arg_b = arg_pool.tile([P, CHUNK], F32, name="arg_b")
+            for arg, tt in ((arg_a, t), (arg_b, t + 1)):
+                nc.vector.tensor_scalar(
+                    out=arg[:], in0=on[(c, tt)][:], scalar1=gain[:, tt : tt + 1], scalar2=1.0,
+                    op0=ALU.mult, op1=ALU.add,
+                )
+            nc.vector.tensor_mul(out=result, in0=arg_a[:], in1=arg_b[:])
+
+        def first_arguments(c):
+            half_product[c] = arg_pool.tile([P, CHUNK], F32, name="half_a")
+            multiply_arguments(c, 0, half_product[c][:])
+
+        def last_arguments(c):
+            other_half = arg_pool.tile([P, CHUNK], F32, name="half_b")
+            multiply_arguments(c, 2, other_half[:])
+            nc.vector.tensor_mul(out=product[:, c, :], in0=half_product[c][:], in1=other_half[:])
+
+        def transpose_pair(first_tile):
+            for i in range(first_tile, min(first_tile + 2, BATCH_TILES)):
+                transpose_x(i)
+
+        transpose_pair(0)
+        transpose_pair(2)
+        quantise(0)
+        transpose_pair(4)
+        for c in range(CHUNKS):
+            for i in range((c + X_AHEAD) * CHUNK_TILES, min((c + X_AHEAD + 1) * CHUNK_TILES, BATCH_TILES)):
+                load_x(i)
+            if c > 0:
+                last_arguments(c - 1)
+            multiply(c, 0)
+            multiply(c, 1)
+            transpose_pair(c * CHUNK_TILES + 6)
+            if c + 1 < CHUNKS:
+                quantise(c + 1)
+            first_arguments(c)
+            multiply(c, 2)
+            multiply(c, 3)
+            transpose_pair(c * CHUNK_TILES + 8)
+        last_arguments(CHUNKS - 1)
+
+        logit_diff = const.tile([P, BATCH_TILES], F32)
+        for c in range(CHUNKS):
+            bank = flip_pool.tile([P, CHUNK_TILES, P], F32, name="bank")
+            for j in range(CHUNK_TILES):
+                nc.tensor.transpose(bank[:, j, :], product[:, c, j * P : (j + 1) * P], ident[:])
+            logs = arg_pool.tile([P, CHUNK_TILES, P], F32, name="logs")
+            nc.scalar.activation(out=logs[:], in_=bank[:], func=ACT.Ln)
+            nc.vector.tensor_reduce(
+                out=logit_diff[:, c * CHUNK_TILES : (c + 1) * CHUNK_TILES], in_=logs[:],
+                axis=mybir.AxisListType.X, op=ALU.add,
+            )
+
+        probs = const.tile([P, BATCH_TILES, 2], F32)
+        nc.scalar.activation(out=probs[:, :, 0], in_=logit_diff[:], func=ACT.Sigmoid, bias=y_diff[:, 0:1])
+        nc.scalar.activation(
+            out=probs[:, :, 1], in_=logit_diff[:], func=ACT.Sigmoid, bias=y_diff_neg[:, 0:1], scale=-1.0
+        )
+        nc.sync.dma_start(
+            out=out.rearrange("(p i) c -> p (i c)", i=BATCH_TILES),
+            in_=probs[:].rearrange("p i c -> p (i c)"),
+        )

@@ -23,6 +23,7 @@ CHUNK_TILES = 4
 CHUNK = CHUNK_TILES * P
 CHUNKS = BATCH_TILES // CHUNK_TILES
 X_AHEAD = 3
+SORTED_AHEAD = 6
 
 FLOPS = 2 * BATCH * VISIBLE * HIDDEN
 
@@ -34,6 +35,7 @@ def tile_rbm_kernel(tc, input_data, W_words, W_scales, U, h_bias, y_bias, out):
     with ExitStack() as stack:
         const = stack.enter_context(tc.tile_pool(name="const", bufs=1))
         x_pool = stack.enter_context(tc.tile_pool(name="x", bufs=X_AHEAD * CHUNK_TILES))
+        sorted_pool = stack.enter_context(tc.tile_pool(name="sorted", bufs=SORTED_AHEAD))
         mx_pool = stack.enter_context(tc.tile_pool(name="mx", bufs=2))
         on_pool = stack.enter_context(tc.tile_pool(name="on", bufs=2 * HID_TILES))
         arg_pool = stack.enter_context(tc.tile_pool(name="arg", bufs=2))
@@ -95,14 +97,17 @@ def tile_rbm_kernel(tc, input_data, W_words, W_scales, U, h_bias, y_bias, out):
         inv_neg = const.tile([P, HID_TILES], F32)
         ratio = const.tile([P, HID_TILES], F32)
         gain = const.tile([P, HID_TILES], F32)
-        nc.vector.reciprocal(out=inv_neg[:], in_=sig_neg[:])
-        nc.vector.tensor_mul(out=ratio[:], in0=sig_pos[:], in1=inv_neg[:])
-        nc.vector.tensor_scalar_add(out=gain[:], in0=ratio[:], scalar1=-1.0)
         y_diff = const.tile([P, 1], F32)
         y_diff_neg = const.tile([P, 1], F32)
-        nc.vector.tensor_sub(out=y_diff[:], in0=y_all[:, 0:1], in1=y_all[:, 1:2])
-        nc.vector.tensor_sub(out=y_diff_neg[:], in0=y_all[:, 1:2], in1=y_all[:, 0:1])
 
+        def finish_constants():
+            nc.vector.reciprocal(out=inv_neg[:], in_=sig_neg[:])
+            nc.vector.tensor_mul(out=ratio[:], in0=sig_pos[:], in1=inv_neg[:])
+            nc.vector.tensor_scalar_add(out=gain[:], in0=ratio[:], scalar1=-1.0)
+            nc.vector.tensor_sub(out=y_diff[:], in0=y_all[:, 0:1], in1=y_all[:, 1:2])
+            nc.vector.tensor_sub(out=y_diff_neg[:], in0=y_all[:, 1:2], in1=y_all[:, 0:1])
+
+        sorted_x = {}
         grouped = {}
         codes = {}
         planes = {}
@@ -110,20 +115,25 @@ def tile_rbm_kernel(tc, input_data, W_words, W_scales, U, h_bias, y_bias, out):
         half_product = {}
         product = const.tile([P, CHUNKS, CHUNK], F32)
 
+        def sort_x(i):
+            if i < BATCH_TILES:
+                sorted_x[i] = sorted_pool.tile([P, PASSES, 2, P], F32, name="sorted_x")
+                nc.vector.tensor_copy(
+                    out=sorted_x[i][:],
+                    in_=x_tiles[i][:].bitcast(F32).rearrange("b (g p u) -> b g u p", g=PASSES, u=2),
+                )
+
         def transpose_x(i):
             c, j = divmod(i, CHUNK_TILES)
             if j == 0:
                 grouped[c] = mx_pool.tile([P, PASSES, 4 * CHUNK], BF16, name="grouped", align_bytes=64)
-            x_words = x_tiles[i][:].bitcast(F32)
             dest = grouped[c][:].bitcast(F32).rearrange("p g (b u) -> p g b u", u=2)
             for half in range(2):
                 bank = flip_pool.tile([P, 2, 2, P], F32, name="bank")
                 for gg in range(2):
-                    first = WORDS * (2 * half + gg)
                     for u in range(2):
-                        nc.tensor.transpose(bank[:, gg, u, :], x_words[:, first + u : first + WORDS : 2], ident[:])
-                copy_out = nc.vector.tensor_copy if (2 * i + half) % 4 == 3 else nc.scalar.copy
-                copy_out(
+                        nc.tensor.transpose(bank[:, gg, u, :], sorted_x[i][:, 2 * half + gg, u, :], ident[:])
+                nc.scalar.copy(
                     out=dest[:, 2 * half : 2 * half + 2, j * P : (j + 1) * P, :],
                     in_=bank[:].rearrange("p g u b -> p g b u"),
                 )
@@ -154,48 +164,65 @@ def tile_rbm_kernel(tc, input_data, W_words, W_scales, U, h_bias, y_bias, out):
             on[(c, t)] = on_pool.tile([P, CHUNK], F32, name="on")
             nc.scalar.activation(out=on[(c, t)][:], in_=acc[:], func=ACT.Sigmoid, bias=sig_bias[:, t : t + 1])
 
-        def multiply_arguments(c, t, result):
-            arg_a = arg_pool.tile([P, CHUNK], F32, name="arg_a")
-            arg_b = arg_pool.tile([P, CHUNK], F32, name="arg_b")
-            for arg, tt in ((arg_a, t), (arg_b, t + 1)):
+        def arguments(c, t):
+            pair = []
+            for tt in (t, t + 1):
+                arg = arg_pool.tile([P, CHUNK], F32, name="arg%d" % (tt - t))
                 nc.vector.tensor_scalar(
                     out=arg[:], in0=on[(c, tt)][:], scalar1=gain[:, tt : tt + 1], scalar2=1.0,
                     op0=ALU.mult, op1=ALU.add,
                 )
-            nc.vector.tensor_mul(out=result, in0=arg_a[:], in1=arg_b[:])
+                pair.append(arg)
+            return pair
 
-        def first_arguments(c):
-            half_product[c] = arg_pool.tile([P, CHUNK], F32, name="half_a")
-            multiply_arguments(c, 0, half_product[c][:])
+        def open_product(c, tile_to_sort):
+            arg_a, arg_b = arguments(c, 0)
+            sort_x(tile_to_sort)
+            half_product[c] = arg_pool.tile([P, CHUNK], F32, name="half_product")
+            nc.vector.tensor_mul(out=half_product[c][:], in0=arg_a[:], in1=arg_b[:])
+            sort_x(tile_to_sort + 1)
 
-        def last_arguments(c):
-            other_half = arg_pool.tile([P, CHUNK], F32, name="half_b")
-            multiply_arguments(c, 2, other_half[:])
+        def close_product(c, tile_to_sort):
+            arg_a, arg_b = arguments(c, 2)
+            sort_x(tile_to_sort)
+            other_half = arg_pool.tile([P, CHUNK], F32, name="other_half")
+            nc.vector.tensor_mul(out=other_half[:], in0=arg_a[:], in1=arg_b[:])
+            sort_x(tile_to_sort + 1)
             nc.vector.tensor_mul(out=product[:, c, :], in0=half_product[c][:], in1=other_half[:])
 
         def transpose_pair(first_tile):
             for i in range(first_tile, min(first_tile + 2, BATCH_TILES)):
                 transpose_x(i)
 
-        transpose_pair(0)
-        transpose_pair(2)
+        for i in range(CHUNK_TILES):
+            sort_x(i)
+            transpose_x(i)
+        sort_x(4)
+        sort_x(5)
         quantise(0)
         transpose_pair(4)
+        sort_x(6)
+        sort_x(7)
+        finish_constants()
         for c in range(CHUNKS):
-            for i in range((c + X_AHEAD) * CHUNK_TILES, min((c + X_AHEAD + 1) * CHUNK_TILES, BATCH_TILES)):
+            tile0 = c * CHUNK_TILES
+            for i in range(tile0 + X_AHEAD * CHUNK_TILES, min(tile0 + (X_AHEAD + 1) * CHUNK_TILES, BATCH_TILES)):
                 load_x(i)
             if c > 0:
-                last_arguments(c - 1)
+                close_product(c - 1, tile0 + 8)
+            else:
+                sort_x(tile0 + 8)
+                sort_x(tile0 + 9)
             multiply(c, 0)
             multiply(c, 1)
-            transpose_pair(c * CHUNK_TILES + 6)
+            transpose_pair(tile0 + 6)
+            open_product(c, tile0 + 10)
             if c + 1 < CHUNKS:
                 quantise(c + 1)
-            first_arguments(c)
             multiply(c, 2)
             multiply(c, 3)
-            transpose_pair(c * CHUNK_TILES + 8)
-        last_arguments(CHUNKS - 1)
+            transpose_pair(tile0 + 8)
+        close_product(CHUNKS - 1, BATCH_TILES)
 
         logit_diff = const.tile([P, BATCH_TILES], F32)
         for c in range(CHUNKS):

@@ -19,28 +19,29 @@ PASSES = VISIBLE // K_PASS
 WORDS = K_PASS // 2
 HID_TILES = HIDDEN // P
 BATCH_TILES = BATCH // P
+PAIR = 2 * P
+PAIRS = BATCH // PAIR
 CHUNK_TILES = 4
 CHUNK = CHUNK_TILES * P
-CHUNKS = BATCH_TILES // CHUNK_TILES
-X_AHEAD = 3
-SORTED_AHEAD = 6
+CHUNKS = BATCH // CHUNK
+X_AHEAD = 6
 
 FLOPS = 2 * BATCH * VISIBLE * HIDDEN
 
 
 def tile_rbm_kernel(tc, input_data, W_words, W_scales, U, h_bias, y_bias, out):
     nc = tc.nc
-    x_by_tile = input_data.rearrange("(p i) k -> i p k", i=BATCH_TILES)
+    x_by_pair = input_data.rearrange("(p n j) k -> n p (j k)", n=PAIRS, j=2)
 
     with ExitStack() as stack:
         const = stack.enter_context(tc.tile_pool(name="const", bufs=1))
-        x_pool = stack.enter_context(tc.tile_pool(name="x", bufs=X_AHEAD * CHUNK_TILES))
-        sorted_pool = stack.enter_context(tc.tile_pool(name="sorted", bufs=SORTED_AHEAD))
-        mx_pool = stack.enter_context(tc.tile_pool(name="mx", bufs=2))
+        x_pool = stack.enter_context(tc.tile_pool(name="x", bufs=X_AHEAD))
+        mx_pool = stack.enter_context(tc.tile_pool(name="mx", bufs=3))
         on_pool = stack.enter_context(tc.tile_pool(name="on", bufs=2 * HID_TILES))
-        arg_pool = stack.enter_context(tc.tile_pool(name="arg", bufs=2))
+        arg_pool = stack.enter_context(tc.tile_pool(name="arg", bufs=HID_TILES))
+        half_pool = stack.enter_context(tc.tile_pool(name="half", bufs=2))
         flip_pool = stack.enter_context(tc.psum_pool(name="flip", bufs=4))
-        acc_pool = stack.enter_context(tc.psum_pool(name="acc", bufs=3))
+        acc_pool = stack.enter_context(tc.psum_pool(name="acc", bufs=HID_TILES))
         stack.enter_context(tc.manual_schedule())
 
         w_planes = const.tile([P, PASSES, HIDDEN], U8, align_bytes=64)
@@ -61,21 +62,22 @@ def tile_rbm_kernel(tc, input_data, W_words, W_scales, U, h_bias, y_bias, out):
         ident = const.tile([P, P], F32)
         make_identity(nc, ident[:])
 
-        x_tiles = {}
+        x_pairs = {}
 
-        def load_x(i):
-            x_tiles[i] = x_pool.tile([P, VISIBLE], BF16, name="x_tile")
-            nc.sync.dma_start(out=x_tiles[i][:], in_=x_by_tile[i])
+        def load_x(n):
+            if n < PAIRS:
+                x_pairs[n] = x_pool.tile([P, 2 * VISIBLE], BF16, name="x_pair")
+                nc.sync.dma_start(out=x_pairs[n][:], in_=x_by_pair[n])
 
         w_codes = const.tile([P, PASSES, HIDDEN], U32, align_bytes=64)
-        for i in range(6):
-            load_x(i)
+        load_x(0)
+        load_x(1)
         nc.sync.dma_start(
             out=w_codes[:].bitcast(I32),
             in_=W_words.rearrange("g p n t -> p g (n t)").bitcast(I32),
         )
-        for i in range(6, X_AHEAD * CHUNK_TILES):
-            load_x(i)
+        for n in range(2, X_AHEAD):
+            load_x(n)
 
         as_rows = const.tile([P, 3, P], F32)
         nc.vector.memset(as_rows[:], 0.0)
@@ -111,125 +113,118 @@ def tile_rbm_kernel(tc, input_data, W_words, W_scales, U, h_bias, y_bias, out):
         grouped = {}
         codes = {}
         planes = {}
+        acc = {}
         on = {}
-        half_product = {}
+        args = {}
+        halves = {}
         product = const.tile([P, CHUNKS, CHUNK], F32)
 
-        def sort_x(i):
-            if i < BATCH_TILES:
-                sorted_x[i] = sorted_pool.tile([P, PASSES, 2, P], F32, name="sorted_x")
+        def sort_x(n):
+            if n < PAIRS:
+                sorted_x[n] = mx_pool.tile([P, 2 * PASSES, 2, P], F32, name="sorted_x")
                 nc.vector.tensor_copy(
-                    out=sorted_x[i][:],
-                    in_=x_tiles[i][:].bitcast(F32).rearrange("b (g p u) -> b g u p", g=PASSES, u=2),
+                    out=sorted_x[n][:],
+                    in_=x_pairs[n][:].bitcast(F32).rearrange("b (s p u) -> b s u p", s=2 * PASSES, u=2),
                 )
 
-        def transpose_x(i):
-            c, j = divmod(i, CHUNK_TILES)
-            if j == 0:
-                grouped[c] = mx_pool.tile([P, PASSES, 4 * CHUNK], BF16, name="grouped", align_bytes=64)
-            dest = grouped[c][:].bitcast(F32).rearrange("p g (b u) -> p g b u", u=2)
-            for half in range(2):
-                bank = flip_pool.tile([P, 2, 2, P], F32, name="bank")
-                for gg in range(2):
-                    for u in range(2):
-                        nc.tensor.transpose(bank[:, gg, u, :], sorted_x[i][:, 2 * half + gg, u, :], ident[:])
-                nc.scalar.copy(
-                    out=dest[:, 2 * half : 2 * half + 2, j * P : (j + 1) * P, :],
-                    in_=bank[:].rearrange("p g u b -> p g b u"),
-                )
+        def transpose_x(n):
+            if n < PAIRS:
+                grouped[n] = mx_pool.tile([P, PASSES, 4 * PAIR], BF16, name="grouped", align_bytes=64)
+                dest = grouped[n][:].bitcast(F32).rearrange("p g (b u) -> p g b u", u=2)
+                for j in range(2):
+                    for g0 in range(0, PASSES, 2):
+                        bank = flip_pool.tile([P, 2, 2, P], F32, name="bank")
+                        for g in range(g0, g0 + 2):
+                            for u in range(2):
+                                nc.tensor.transpose(bank[:, g - g0, u, :], sorted_x[n][:, PASSES * j + g, u, :], ident[:])
+                        nc.scalar.copy(
+                            out=dest[:, g0 : g0 + 2, j * P : (j + 1) * P, :],
+                            in_=bank[:].rearrange("p g u b -> p g b u"),
+                        )
 
-        def quantise(c):
-            codes[c] = mx_pool.tile([P, PASSES, CHUNK], U32, name="codes", align_bytes=64)
-            planes[c] = mx_pool.tile([P, PASSES, CHUNK], U8, name="planes", align_bytes=64)
-            for g in range(PASSES):
+        def quantise(n):
+            if n < PAIRS:
+                codes[n] = mx_pool.tile([P, PASSES, PAIR], U32, name="codes", align_bytes=64)
+                planes[n] = mx_pool.tile([P, PASSES, PAIR], U8, name="planes", align_bytes=64)
                 nc.vector.quantize_mx(
-                    out=codes[c][:, g, :].bitcast(FP8X4),
-                    scales=planes[c][:, g, :],
-                    in_=grouped[c][:, g, :],
+                    out=codes[n][:].rearrange("p g b -> p (g b)").bitcast(FP8X4),
+                    scales=planes[n][:].rearrange("p g b -> p (g b)"),
+                    in_=grouped[n][:].rearrange("p g w -> p (g w)"),
                 )
 
-        def multiply(c, t):
-            hid = slice(t * P, (t + 1) * P)
-            acc = acc_pool.tile([P, CHUNK], F32, name="acc")
-            for g in range(PASSES):
-                nc.tensor.matmul_mx(
-                    out=acc[:],
-                    lhsT=w_codes[:, g, hid].bitcast(FP8X4),
-                    lhsT_scale=w_planes[:, g, hid],
-                    rhs=codes[c][:, g, :].bitcast(FP8X4),
-                    rhs_scale=planes[c][:, g, :],
-                    start=(g == 0),
-                    stop=(g == PASSES - 1),
-                )
-            on[(c, t)] = on_pool.tile([P, CHUNK], F32, name="on")
-            nc.scalar.activation(out=on[(c, t)][:], in_=acc[:], func=ACT.Sigmoid, bias=sig_bias[:, t : t + 1])
+        def multiply(n):
+            c, second = divmod(n, 2)
+            for t in range(HID_TILES):
+                if not second:
+                    acc[(c, t)] = acc_pool.tile([P, CHUNK], F32, name="acc")
+                hid = slice(t * P, (t + 1) * P)
+                for g in range(PASSES):
+                    nc.tensor.matmul_mx(
+                        out=acc[(c, t)][:, second * PAIR : (second + 1) * PAIR],
+                        lhsT=w_codes[:, g, hid].bitcast(FP8X4),
+                        lhsT_scale=w_planes[:, g, hid],
+                        rhs=codes[n][:, g, :].bitcast(FP8X4),
+                        rhs_scale=planes[n][:, g, :],
+                        start=(g == 0),
+                        stop=(g == PASSES - 1),
+                    )
+                if second:
+                    on[(c, t)] = on_pool.tile([P, CHUNK], F32, name="on")
+                    nc.scalar.activation(
+                        out=on[(c, t)][:], in_=acc[(c, t)][:], func=ACT.Sigmoid, bias=sig_bias[:, t : t + 1]
+                    )
 
-        def arguments(c, t):
-            pair = []
-            for tt in (t, t + 1):
-                arg = arg_pool.tile([P, CHUNK], F32, name="arg%d" % (tt - t))
+        def arguments(c):
+            for t in range(HID_TILES):
+                args[(c, t)] = arg_pool.tile([P, CHUNK], F32, name="arg")
                 nc.vector.tensor_scalar(
-                    out=arg[:], in0=on[(c, tt)][:], scalar1=gain[:, tt : tt + 1], scalar2=1.0,
+                    out=args[(c, t)][:], in0=on[(c, t)][:], scalar1=gain[:, t : t + 1], scalar2=1.0,
                     op0=ALU.mult, op1=ALU.add,
                 )
-                pair.append(arg)
-            return pair
 
-        def open_product(c, tile_to_sort):
-            arg_a, arg_b = arguments(c, 0)
-            sort_x(tile_to_sort)
-            half_product[c] = arg_pool.tile([P, CHUNK], F32, name="half_product")
-            nc.vector.tensor_mul(out=half_product[c][:], in0=arg_a[:], in1=arg_b[:])
-            sort_x(tile_to_sort + 1)
+        def half_product(c, t):
+            halves[(c, t)] = half_pool.tile([P, CHUNK], F32, name="half%d" % t)
+            nc.vector.tensor_mul(out=halves[(c, t)][:], in0=args[(c, t)][:], in1=args[(c, t + 1)][:])
 
-        def close_product(c, tile_to_sort):
-            arg_a, arg_b = arguments(c, 2)
-            sort_x(tile_to_sort)
-            other_half = arg_pool.tile([P, CHUNK], F32, name="other_half")
-            nc.vector.tensor_mul(out=other_half[:], in0=arg_a[:], in1=arg_b[:])
-            sort_x(tile_to_sort + 1)
-            nc.vector.tensor_mul(out=product[:, c, :], in0=half_product[c][:], in1=other_half[:])
+        def whole_product(c):
+            nc.vector.tensor_mul(out=product[:, c, :], in0=halves[(c, 0)][:], in1=halves[(c, 2)][:])
 
-        def transpose_pair(first_tile):
-            for i in range(first_tile, min(first_tile + 2, BATCH_TILES)):
-                transpose_x(i)
-
-        for i in range(CHUNK_TILES):
-            sort_x(i)
-            transpose_x(i)
-        sort_x(4)
-        sort_x(5)
+        sort_x(0)
+        transpose_x(0)
+        sort_x(1)
+        transpose_x(1)
         quantise(0)
-        transpose_pair(4)
-        sort_x(6)
-        sort_x(7)
+        sort_x(2)
         finish_constants()
         for c in range(CHUNKS):
-            tile0 = c * CHUNK_TILES
-            for i in range(tile0 + X_AHEAD * CHUNK_TILES, min(tile0 + (X_AHEAD + 1) * CHUNK_TILES, BATCH_TILES)):
-                load_x(i)
+            load_x(2 * c + X_AHEAD)
+            load_x(2 * c + X_AHEAD + 1)
             if c > 0:
-                close_product(c - 1, tile0 + 8)
-            else:
-                sort_x(tile0 + 8)
-                sort_x(tile0 + 9)
-            multiply(c, 0)
-            multiply(c, 1)
-            transpose_pair(tile0 + 6)
-            open_product(c, tile0 + 10)
-            if c + 1 < CHUNKS:
-                quantise(c + 1)
-            multiply(c, 2)
-            multiply(c, 3)
-            transpose_pair(tile0 + 8)
-        close_product(CHUNKS - 1, BATCH_TILES)
+                arguments(c - 1)
+                half_product(c - 1, 0)
+            quantise(2 * c + 1)
+            multiply(2 * c)
+            if c > 0:
+                half_product(c - 1, 2)
+            sort_x(2 * c + 3)
+            if c > 0:
+                whole_product(c - 1)
+            transpose_x(2 * c + 2)
+            quantise(2 * c + 2)
+            sort_x(2 * c + 4)
+            multiply(2 * c + 1)
+            transpose_x(2 * c + 3)
+        arguments(CHUNKS - 1)
+        half_product(CHUNKS - 1, 0)
+        half_product(CHUNKS - 1, 2)
+        whole_product(CHUNKS - 1)
 
         logit_diff = const.tile([P, BATCH_TILES], F32)
         for c in range(CHUNKS):
             bank = flip_pool.tile([P, CHUNK_TILES, P], F32, name="bank")
             for j in range(CHUNK_TILES):
                 nc.tensor.transpose(bank[:, j, :], product[:, c, j * P : (j + 1) * P], ident[:])
-            logs = arg_pool.tile([P, CHUNK_TILES, P], F32, name="logs")
+            logs = half_pool.tile([P, CHUNK_TILES, P], F32, name="logs")
             nc.scalar.activation(out=logs[:], in_=bank[:], func=ACT.Ln)
             nc.vector.tensor_reduce(
                 out=logit_diff[:, c * CHUNK_TILES : (c + 1) * CHUNK_TILES], in_=logs[:],

@@ -25,6 +25,7 @@ CHUNK_TILES = 4
 CHUNK = CHUNK_TILES * P
 CHUNKS = BATCH // CHUNK
 X_AHEAD = 6
+TINY = 2.0 ** -30
 
 FLOPS = 2 * BATCH * VISIBLE * HIDDEN
 
@@ -38,8 +39,7 @@ def tile_rbm_kernel(tc, input_data, W_words, W_scales, U, h_bias, y_bias, out):
         x_pool = stack.enter_context(tc.tile_pool(name="x", bufs=X_AHEAD))
         mx_pool = stack.enter_context(tc.tile_pool(name="mx", bufs=3))
         on_pool = stack.enter_context(tc.tile_pool(name="on", bufs=2 * HID_TILES))
-        arg_pool = stack.enter_context(tc.tile_pool(name="arg", bufs=HID_TILES))
-        half_pool = stack.enter_context(tc.tile_pool(name="half", bufs=2))
+        run_pool = stack.enter_context(tc.tile_pool(name="run", bufs=2))
         flip_pool = stack.enter_context(tc.psum_pool(name="flip", bufs=4))
         acc_pool = stack.enter_context(tc.psum_pool(name="acc", bufs=HID_TILES))
         stack.enter_context(tc.manual_schedule())
@@ -99,6 +99,11 @@ def tile_rbm_kernel(tc, input_data, W_words, W_scales, U, h_bias, y_bias, out):
         inv_neg = const.tile([P, HID_TILES], F32)
         ratio = const.tile([P, HID_TILES], F32)
         gain = const.tile([P, HID_TILES], F32)
+        nudge = const.tile([P, HID_TILES], F32)
+        factor = const.tile([P, HID_TILES], F32)
+        shift = const.tile([P, HID_TILES], F32)
+        factor_pairs = const.tile([P, 2], F32)
+        factor_all = const.tile([P, 1], F32)
         y_diff = const.tile([P, 1], F32)
         y_diff_neg = const.tile([P, 1], F32)
 
@@ -106,8 +111,15 @@ def tile_rbm_kernel(tc, input_data, W_words, W_scales, U, h_bias, y_bias, out):
             nc.vector.reciprocal(out=inv_neg[:], in_=sig_neg[:])
             nc.vector.tensor_mul(out=ratio[:], in0=sig_pos[:], in1=inv_neg[:])
             nc.vector.tensor_scalar_add(out=gain[:], in0=ratio[:], scalar1=-1.0)
+            nc.vector.tensor_scalar(
+                out=nudge[:], in0=gain[:], scalar1=0.0, scalar2=TINY, op0=ALU.is_equal, op1=ALU.mult
+            )
             nc.vector.tensor_sub(out=y_diff[:], in0=y_all[:, 0:1], in1=y_all[:, 1:2])
+            nc.vector.tensor_add(out=factor[:], in0=gain[:], in1=nudge[:])
             nc.vector.tensor_sub(out=y_diff_neg[:], in0=y_all[:, 1:2], in1=y_all[:, 0:1])
+            nc.vector.reciprocal(out=shift[:], in_=factor[:])
+            nc.vector.tensor_mul(out=factor_pairs[:], in0=factor[:, 0:2], in1=factor[:, 2:4])
+            nc.vector.tensor_mul(out=factor_all[:], in0=factor_pairs[:, 0:1], in1=factor_pairs[:, 1:2])
 
         sorted_x = {}
         grouped = {}
@@ -115,8 +127,7 @@ def tile_rbm_kernel(tc, input_data, W_words, W_scales, U, h_bias, y_bias, out):
         planes = {}
         acc = {}
         on = {}
-        args = {}
-        halves = {}
+        running = {}
         product = const.tile([P, CHUNKS, CHUNK], F32)
 
         def sort_x(n):
@@ -174,20 +185,23 @@ def tile_rbm_kernel(tc, input_data, W_words, W_scales, U, h_bias, y_bias, out):
                         out=on[(c, t)][:], in_=acc[(c, t)][:], func=ACT.Sigmoid, bias=sig_bias[:, t : t + 1]
                     )
 
-        def arguments(c):
-            for t in range(HID_TILES):
-                args[(c, t)] = arg_pool.tile([P, CHUNK], F32, name="arg")
+        def extend_product(c, t):
+            if t == 0:
+                running[(c, 0)] = run_pool.tile([P, CHUNK], F32, name="run0")
                 nc.vector.tensor_scalar(
-                    out=args[(c, t)][:], in0=on[(c, t)][:], scalar1=gain[:, t : t + 1], scalar2=1.0,
-                    op0=ALU.mult, op1=ALU.add,
+                    out=running[(c, 0)][:], in0=on[(c, 0)][:], scalar1=shift[:, 0:1], scalar2=factor_all[:, 0:1],
+                    op0=ALU.add, op1=ALU.mult,
                 )
-
-        def half_product(c, t):
-            halves[(c, t)] = half_pool.tile([P, CHUNK], F32, name="half%d" % t)
-            nc.vector.tensor_mul(out=halves[(c, t)][:], in0=args[(c, t)][:], in1=args[(c, t + 1)][:])
-
-        def whole_product(c):
-            nc.vector.tensor_mul(out=product[:, c, :], in0=halves[(c, 0)][:], in1=halves[(c, 2)][:])
+                return
+            if t < HID_TILES - 1:
+                running[(c, t)] = run_pool.tile([P, CHUNK], F32, name="run%d" % t)
+                dest = running[(c, t)][:]
+            else:
+                dest = product[:, c, :]
+            nc.vector.scalar_tensor_tensor(
+                out=dest, in0=on[(c, t)][:], scalar=shift[:, t : t + 1], in1=running[(c, t - 1)][:],
+                op0=ALU.add, op1=ALU.mult,
+            )
 
         sort_x(0)
         transpose_x(0)
@@ -200,31 +214,30 @@ def tile_rbm_kernel(tc, input_data, W_words, W_scales, U, h_bias, y_bias, out):
             load_x(2 * c + X_AHEAD)
             load_x(2 * c + X_AHEAD + 1)
             if c > 0:
-                arguments(c - 1)
-                half_product(c - 1, 0)
+                extend_product(c - 1, 0)
+            sort_x(2 * c + 3)
+            if c > 0:
+                extend_product(c - 1, 1)
             quantise(2 * c + 1)
             multiply(2 * c)
             if c > 0:
-                half_product(c - 1, 2)
-            sort_x(2 * c + 3)
-            if c > 0:
-                whole_product(c - 1)
+                extend_product(c - 1, 2)
             transpose_x(2 * c + 2)
-            quantise(2 * c + 2)
             sort_x(2 * c + 4)
+            if c > 0:
+                extend_product(c - 1, 3)
+            quantise(2 * c + 2)
             multiply(2 * c + 1)
             transpose_x(2 * c + 3)
-        arguments(CHUNKS - 1)
-        half_product(CHUNKS - 1, 0)
-        half_product(CHUNKS - 1, 2)
-        whole_product(CHUNKS - 1)
+        for t in range(HID_TILES):
+            extend_product(CHUNKS - 1, t)
 
         logit_diff = const.tile([P, BATCH_TILES], F32)
         for c in range(CHUNKS):
             bank = flip_pool.tile([P, CHUNK_TILES, P], F32, name="bank")
             for j in range(CHUNK_TILES):
                 nc.tensor.transpose(bank[:, j, :], product[:, c, j * P : (j + 1) * P], ident[:])
-            logs = half_pool.tile([P, CHUNK_TILES, P], F32, name="logs")
+            logs = run_pool.tile([P, CHUNK_TILES, P], F32, name="logs")
             nc.scalar.activation(out=logs[:], in_=bank[:], func=ACT.Ln)
             nc.vector.tensor_reduce(
                 out=logit_diff[:, c * CHUNK_TILES : (c + 1) * CHUNK_TILES], in_=logs[:],

@@ -32,7 +32,7 @@ FLOPS = 2 * BATCH * VISIBLE * HIDDEN
 
 def tile_rbm_kernel(tc, input_data, W_words, W_scales, U, h_bias, y_bias, out):
     nc = tc.nc
-    x_by_pair = input_data.rearrange("(p n j) k -> n p (j k)", n=PAIRS, j=2)
+    x_by_half = input_data.rearrange("(p c j) (h k) -> c h p j k", c=CHUNKS, j=CHUNK_TILES, h=2)
 
     with ExitStack() as stack:
         const = stack.enter_context(tc.tile_pool(name="const", bufs=1))
@@ -44,6 +44,32 @@ def tile_rbm_kernel(tc, input_data, W_words, W_scales, U, h_bias, y_bias, out):
         acc_pool = stack.enter_context(tc.psum_pool(name="acc", bufs=HID_TILES))
         stack.enter_context(tc.manual_schedule())
 
+        h_rows = const.tile([HID_TILES, P], BF16)
+        u_rows = const.tile([HID_TILES, P, 2], BF16)
+        y_all = const.tile([P, 2], BF16)
+        nc.scalar.dma_start(out=h_rows[:], in_=h_bias.rearrange("o (t p) -> (o t) p", p=P))
+        nc.scalar.dma_start(out=u_rows[:], in_=U.rearrange("(t p) c -> t p c", p=P))
+        nc.scalar.dma_start(out=y_all[:], in_=y_bias.rearrange("o c -> (o c)").partition_broadcast(P))
+        warm = const.tile([P, 2], F32)
+        nc.vector.memset(warm[:, 0:1], 0.0)
+        nc.scalar.activation(out=warm[:, 1:2], in_=warm[:, 0:1], func=ACT.Sigmoid)
+
+        ident = const.tile([P, P], F32)
+        make_identity(nc, ident[:])
+
+        x_pairs = {}
+
+        def load_x(n, pieces=1):
+            if n < PAIRS:
+                x_pairs[n] = x_pool.tile([P, CHUNK_TILES, VISIBLE // 2], BF16, name="x_pair")
+                count = CHUNK_TILES // pieces
+                for i in range(pieces):
+                    rows = slice(i * count, (i + 1) * count)
+                    nc.sync.dma_start(out=x_pairs[n][:, rows, :], in_=x_by_half[n // 2][n % 2][:, rows, :])
+
+        w_codes = const.tile([P, PASSES, HIDDEN], U32, align_bytes=64)
+        load_x(0, pieces=2)
+        load_x(1, pieces=2)
         w_planes = const.tile([P, PASSES, HIDDEN], U8, align_bytes=64)
         nc.vector.memset(w_planes[:].bitcast(I32), 0)
         for quad in range(4):
@@ -52,26 +78,6 @@ def tile_rbm_kernel(tc, input_data, W_words, W_scales, U, h_bias, y_bias, out):
                 in_=W_scales[:, 4 * quad : 4 * quad + 4, :].rearrange("g r n -> r g n").bitcast(I32),
             )
 
-        h_rows = const.tile([HID_TILES, P], BF16)
-        u_rows = const.tile([HID_TILES, P, 2], BF16)
-        y_all = const.tile([P, 2], BF16)
-        nc.scalar.dma_start(out=h_rows[:], in_=h_bias.rearrange("o (t p) -> (o t) p", p=P))
-        nc.scalar.dma_start(out=u_rows[:], in_=U.rearrange("(t p) c -> t p c", p=P))
-        nc.scalar.dma_start(out=y_all[:], in_=y_bias.rearrange("o c -> (o c)").partition_broadcast(P))
-
-        ident = const.tile([P, P], F32)
-        make_identity(nc, ident[:])
-
-        x_pairs = {}
-
-        def load_x(n):
-            if n < PAIRS:
-                x_pairs[n] = x_pool.tile([P, 2 * VISIBLE], BF16, name="x_pair")
-                nc.sync.dma_start(out=x_pairs[n][:], in_=x_by_pair[n])
-
-        w_codes = const.tile([P, PASSES, HIDDEN], U32, align_bytes=64)
-        load_x(0)
-        load_x(1)
         nc.sync.dma_start(
             out=w_codes[:].bitcast(I32),
             in_=W_words.rearrange("g p n t -> p g (n t)").bitcast(I32),
@@ -81,21 +87,11 @@ def tile_rbm_kernel(tc, input_data, W_words, W_scales, U, h_bias, y_bias, out):
 
         as_rows = const.tile([P, 3, P], F32)
         nc.vector.memset(as_rows[:], 0.0)
-        nc.vector.tensor_copy(out=as_rows[0:HID_TILES, 0, :], in_=h_rows[:])
-        nc.vector.tensor_copy(out=as_rows[0:HID_TILES, 1:3, :], in_=u_rows[:].rearrange("t p c -> t c p"))
-        as_cols_ps = acc_pool.tile([P, 3, P], F32, name="acc")
-        for m in range(3):
-            nc.tensor.transpose(as_cols_ps[:, m, :], as_rows[:, m, :], ident[:])
         as_cols = const.tile([P, 3, HID_TILES], F32)
-        nc.vector.tensor_copy(out=as_cols[:], in_=as_cols_ps[:, :, 0:HID_TILES])
         sig_bias = const.tile([P, HID_TILES], F32)
         u_diff = const.tile([P, HID_TILES], F32)
-        nc.vector.tensor_add(out=sig_bias[:], in0=as_cols[:, 0, :], in1=as_cols[:, 2, :])
-        nc.vector.tensor_sub(out=u_diff[:], in0=as_cols[:, 1, :], in1=as_cols[:, 2, :])
         sig_pos = const.tile([P, HID_TILES], F32)
         sig_neg = const.tile([P, HID_TILES], F32)
-        nc.scalar.activation(out=sig_pos[:], in_=u_diff[:], func=ACT.Sigmoid)
-        nc.scalar.activation(out=sig_neg[:], in_=u_diff[:], func=ACT.Sigmoid, scale=-1.0)
         inv_neg = const.tile([P, HID_TILES], F32)
         ratio = const.tile([P, HID_TILES], F32)
         gain = const.tile([P, HID_TILES], F32)
@@ -106,6 +102,21 @@ def tile_rbm_kernel(tc, input_data, W_words, W_scales, U, h_bias, y_bias, out):
         factor_all = const.tile([P, 1], F32)
         y_diff = const.tile([P, 1], F32)
         y_diff_neg = const.tile([P, 1], F32)
+
+        def constants_onto_partitions():
+            nc.vector.tensor_copy(out=as_rows[0:HID_TILES, 0, :], in_=h_rows[:])
+            nc.vector.tensor_copy(out=as_rows[0:HID_TILES, 1:3, :], in_=u_rows[:].rearrange("t p c -> t c p"))
+            as_cols_ps = acc_pool.tile([P, 3, P], F32, name="acc")
+            for m in range(3):
+                nc.tensor.transpose(as_cols_ps[:, m, :], as_rows[:, m, :], ident[:])
+            return as_cols_ps
+
+        def bias_and_difference(as_cols_ps):
+            nc.vector.tensor_copy(out=as_cols[:], in_=as_cols_ps[:, :, 0:HID_TILES])
+            nc.vector.tensor_add(out=sig_bias[:], in0=as_cols[:, 0, :], in1=as_cols[:, 2, :])
+            nc.vector.tensor_sub(out=u_diff[:], in0=as_cols[:, 1, :], in1=as_cols[:, 2, :])
+            nc.scalar.activation(out=sig_pos[:], in_=u_diff[:], func=ACT.Sigmoid)
+            nc.scalar.activation(out=sig_neg[:], in_=u_diff[:], func=ACT.Sigmoid, scale=-1.0)
 
         def finish_constants():
             nc.vector.reciprocal(out=inv_neg[:], in_=sig_neg[:])
@@ -130,33 +141,35 @@ def tile_rbm_kernel(tc, input_data, W_words, W_scales, U, h_bias, y_bias, out):
         running = {}
         product = const.tile([P, CHUNKS, CHUNK], F32)
 
-        def sort_x(n):
+        def sort_x(n, pieces=1):
             if n < PAIRS:
                 sorted_x[n] = mx_pool.tile([P, 2 * PASSES, 2, P], F32, name="sorted_x")
-                nc.vector.tensor_copy(
-                    out=sorted_x[n][:],
-                    in_=x_pairs[n][:].bitcast(F32).rearrange("b (s p u) -> b s u p", s=2 * PASSES, u=2),
+                words = (
+                    x_pairs[n][:].rearrange("b j k -> b (j k)").bitcast(F32).rearrange("b (s p u) -> b s u p", s=2 * PASSES, u=2)
                 )
+                count = 2 * PASSES // pieces
+                for i in range(pieces):
+                    part = slice(i * count, (i + 1) * count)
+                    nc.vector.tensor_copy(out=sorted_x[n][:, part], in_=words[:, part])
 
         def transpose_x(n):
             if n < PAIRS:
-                grouped[n] = mx_pool.tile([P, PASSES, 4 * PAIR], BF16, name="grouped", align_bytes=64)
+                grouped[n] = mx_pool.tile([P, 2, 4 * CHUNK], BF16, name="grouped", align_bytes=64)
                 dest = grouped[n][:].bitcast(F32).rearrange("p g (b u) -> p g b u", u=2)
-                for j in range(2):
-                    for g0 in range(0, PASSES, 2):
-                        bank = flip_pool.tile([P, 2, 2, P], F32, name="bank")
-                        for g in range(g0, g0 + 2):
-                            for u in range(2):
-                                nc.tensor.transpose(bank[:, g - g0, u, :], sorted_x[n][:, PASSES * j + g, u, :], ident[:])
-                        nc.scalar.copy(
-                            out=dest[:, g0 : g0 + 2, j * P : (j + 1) * P, :],
-                            in_=bank[:].rearrange("p g u b -> p g b u"),
-                        )
+                for j in range(CHUNK_TILES):
+                    bank = flip_pool.tile([P, 2, 2, P], F32, name="bank")
+                    for g in range(2):
+                        for u in range(2):
+                            nc.tensor.transpose(bank[:, g, u, :], sorted_x[n][:, 2 * j + g, u, :], ident[:])
+                    nc.scalar.copy(
+                        out=dest[:, :, j * P : (j + 1) * P, :],
+                        in_=bank[:].rearrange("p g u b -> p g b u"),
+                    )
 
         def quantise(n):
             if n < PAIRS:
-                codes[n] = mx_pool.tile([P, PASSES, PAIR], U32, name="codes", align_bytes=64)
-                planes[n] = mx_pool.tile([P, PASSES, PAIR], U8, name="planes", align_bytes=64)
+                codes[n] = mx_pool.tile([P, 2, CHUNK], U32, name="codes", align_bytes=64)
+                planes[n] = mx_pool.tile([P, 2, CHUNK], U8, name="planes", align_bytes=64)
                 nc.vector.quantize_mx(
                     out=codes[n][:].rearrange("p g b -> p (g b)").bitcast(FP8X4),
                     scales=planes[n][:].rearrange("p g b -> p (g b)"),
@@ -169,15 +182,15 @@ def tile_rbm_kernel(tc, input_data, W_words, W_scales, U, h_bias, y_bias, out):
                 if not second:
                     acc[(c, t)] = acc_pool.tile([P, CHUNK], F32, name="acc")
                 hid = slice(t * P, (t + 1) * P)
-                for g in range(PASSES):
+                for g in range(2):
                     nc.tensor.matmul_mx(
-                        out=acc[(c, t)][:, second * PAIR : (second + 1) * PAIR],
-                        lhsT=w_codes[:, g, hid].bitcast(FP8X4),
-                        lhsT_scale=w_planes[:, g, hid],
+                        out=acc[(c, t)][:],
+                        lhsT=w_codes[:, 2 * second + g, hid].bitcast(FP8X4),
+                        lhsT_scale=w_planes[:, 2 * second + g, hid],
                         rhs=codes[n][:, g, :].bitcast(FP8X4),
                         rhs_scale=planes[n][:, g, :],
-                        start=(g == 0),
-                        stop=(g == PASSES - 1),
+                        start=(not second and g == 0),
+                        stop=(second == 1 and g == 1),
                     )
                 if second:
                     on[(c, t)] = on_pool.tile([P, CHUNK], F32, name="on")
@@ -203,30 +216,33 @@ def tile_rbm_kernel(tc, input_data, W_words, W_scales, U, h_bias, y_bias, out):
                 op0=ALU.add, op1=ALU.mult,
             )
 
-        sort_x(0)
+        sort_x(0, pieces=2)
         transpose_x(0)
-        sort_x(1)
+        sort_x(1, pieces=2)
         transpose_x(1)
+        columns = constants_onto_partitions()
         quantise(0)
+        bias_and_difference(columns)
         sort_x(2)
-        finish_constants()
         for c in range(CHUNKS):
             load_x(2 * c + X_AHEAD)
             load_x(2 * c + X_AHEAD + 1)
             if c > 0:
                 extend_product(c - 1, 0)
-            sort_x(2 * c + 3)
-            if c > 0:
-                extend_product(c - 1, 1)
             quantise(2 * c + 1)
             multiply(2 * c)
             if c > 0:
+                extend_product(c - 1, 1)
+            sort_x(2 * c + 3)
+            if c > 0:
                 extend_product(c - 1, 2)
             transpose_x(2 * c + 2)
-            sort_x(2 * c + 4)
+            quantise(2 * c + 2)
             if c > 0:
                 extend_product(c - 1, 3)
-            quantise(2 * c + 2)
+            sort_x(2 * c + 4)
+            if c == 0:
+                finish_constants()
             multiply(2 * c + 1)
             transpose_x(2 * c + 3)
         for t in range(HID_TILES):

@@ -25,6 +25,7 @@ CHUNK_TILES = 4
 CHUNK = CHUNK_TILES * P
 CHUNKS = BATCH // CHUNK
 X_AHEAD = 6
+VECTOR_BANKS = 1
 TINY = 2.0 ** -30
 
 FLOPS = 2 * BATCH * VISIBLE * HIDDEN
@@ -161,10 +162,16 @@ def tile_rbm_kernel(tc, input_data, W_words, W_scales, U, h_bias, y_bias, out):
                     for g in range(2):
                         for u in range(2):
                             nc.tensor.transpose(bank[:, g, u, :], sorted_x[n][:, 2 * j + g, u, :], ident[:])
-                    nc.scalar.copy(
-                        out=dest[:, :, j * P : (j + 1) * P, :],
-                        in_=bank[:].rearrange("p g u b -> p g b u"),
-                    )
+                    if n % 2 == 1 and j < VECTOR_BANKS:
+                        nc.vector.tensor_copy(
+                            out=dest[:, :, j * P : (j + 1) * P, :],
+                            in_=bank[:].rearrange("p g u b -> p g b u"),
+                        )
+                    else:
+                        nc.scalar.copy(
+                            out=dest[:, :, j * P : (j + 1) * P, :],
+                            in_=bank[:].rearrange("p g u b -> p g b u"),
+                        )
 
         def quantise(n):
             if n < PAIRS:

@@ -68,10 +68,10 @@ def tile_rbm_kernel(tc, input_data, W_words, W_scales, U, h_bias, y_bias, out):
                     rows = slice(i * count, (i + 1) * count)
                     nc.sync.dma_start(out=x_pairs[n][:, rows, :], in_=x_by_half[n // 2][n % 2][:, rows, :])
 
-        w_codes = const.tile([P, PASSES, HIDDEN], U32, align_bytes=64)
+        w_codes = const.tile([P, PASSES, HIDDEN], U32, align_bytes=256)
         load_x(0, pieces=2)
         load_x(1, pieces=2)
-        w_planes = const.tile([P, PASSES, HIDDEN], U8, align_bytes=64)
+        w_planes = const.tile([P, PASSES, HIDDEN], U8, align_bytes=256)
         nc.vector.memset(w_planes[:].bitcast(I32), 0)
         for quad in range(4):
             nc.sync.dma_start(
@@ -155,7 +155,7 @@ def tile_rbm_kernel(tc, input_data, W_words, W_scales, U, h_bias, y_bias, out):
 
         def transpose_x(n):
             if n < PAIRS:
-                grouped[n] = mx_pool.tile([P, 2, 4 * CHUNK], BF16, name="grouped", align_bytes=64)
+                grouped[n] = mx_pool.tile([P, 2, 4 * CHUNK], BF16, name="grouped", align_bytes=256)
                 dest = grouped[n][:].bitcast(F32).rearrange("p g (b u) -> p g b u", u=2)
                 for j in range(CHUNK_TILES):
                     bank = flip_pool.tile([P, 2, 2, P], F32, name="bank")
@@ -175,8 +175,8 @@ def tile_rbm_kernel(tc, input_data, W_words, W_scales, U, h_bias, y_bias, out):
 
         def quantise(n):
             if n < PAIRS:
-                codes[n] = mx_pool.tile([P, 2, CHUNK], U32, name="codes", align_bytes=64)
-                planes[n] = mx_pool.tile([P, 2, CHUNK], U8, name="planes", align_bytes=64)
+                codes[n] = mx_pool.tile([P, 2, CHUNK], U32, name="codes", align_bytes=256)
+                planes[n] = mx_pool.tile([P, 2, CHUNK], U8, name="planes", align_bytes=256)
                 nc.vector.quantize_mx(
                     out=codes[n][:].rearrange("p g b -> p (g b)").bitcast(FP8X4),
                     scales=planes[n][:].rearrange("p g b -> p (g b)"),

@@ -55,14 +55,14 @@ def tile_rbm_kernel(tc, input_data, W_words, W_scales, U, h_bias, y_bias, out):
         nc.vector.memset(warm[:, 0:1], 0.0)
         nc.scalar.activation(out=warm[:, 1:2], in_=warm[:, 0:1], func=ACT.Sigmoid)
 
-        ident = const.tile([P, P], F32)
+        ident = const.tile([P, P], F32, align_bytes=256)
         make_identity(nc, ident[:])
 
         x_pairs = {}
 
         def load_x(n, pieces=1):
             if n < PAIRS:
-                x_pairs[n] = x_pool.tile([P, CHUNK_TILES, VISIBLE // 2], BF16, name="x_pair")
+                x_pairs[n] = x_pool.tile([P, CHUNK_TILES, VISIBLE // 2], BF16, name="x_pair", align_bytes=256)
                 count = CHUNK_TILES // pieces
                 for i in range(pieces):
                     rows = slice(i * count, (i + 1) * count)
@@ -140,11 +140,11 @@ def tile_rbm_kernel(tc, input_data, W_words, W_scales, U, h_bias, y_bias, out):
         acc = {}
         on = {}
         running = {}
-        product = const.tile([P, CHUNKS, CHUNK], F32)
+        product = const.tile([P, CHUNKS, CHUNK], F32, align_bytes=256)
 
         def sort_x(n, pieces=1):
             if n < PAIRS:
-                sorted_x[n] = mx_pool.tile([P, 2 * PASSES, 2, P], F32, name="sorted_x")
+                sorted_x[n] = mx_pool.tile([P, 2 * PASSES, 2, P], F32, name="sorted_x", align_bytes=256)
                 words = (
                     x_pairs[n][:].rearrange("b j k -> b (j k)").bitcast(F32).rearrange("b (s p u) -> b s u p", s=2 * PASSES, u=2)
                 )
@@ -200,21 +200,21 @@ def tile_rbm_kernel(tc, input_data, W_words, W_scales, U, h_bias, y_bias, out):
                         stop=(second == 1 and g == 1),
                     )
                 if second:
-                    on[(c, t)] = on_pool.tile([P, CHUNK], F32, name="on")
+                    on[(c, t)] = on_pool.tile([P, CHUNK], F32, name="on", align_bytes=256)
                     nc.scalar.activation(
                         out=on[(c, t)][:], in_=acc[(c, t)][:], func=ACT.Sigmoid, bias=sig_bias[:, t : t + 1]
                     )
 
         def extend_product(c, t):
             if t == 0:
-                running[(c, 0)] = run_pool.tile([P, CHUNK], F32, name="run0")
+                running[(c, 0)] = run_pool.tile([P, CHUNK], F32, name="run0", align_bytes=256)
                 nc.vector.tensor_scalar(
                     out=running[(c, 0)][:], in0=on[(c, 0)][:], scalar1=shift[:, 0:1], scalar2=factor_all[:, 0:1],
                     op0=ALU.add, op1=ALU.mult,
                 )
                 return
             if t < HID_TILES - 1:
-                running[(c, t)] = run_pool.tile([P, CHUNK], F32, name="run%d" % t)
+                running[(c, t)] = run_pool.tile([P, CHUNK], F32, name="run%d" % t, align_bytes=256)
                 dest = running[(c, t)][:]
             else:
                 dest = product[:, c, :]
@@ -260,7 +260,7 @@ def tile_rbm_kernel(tc, input_data, W_words, W_scales, U, h_bias, y_bias, out):
             bank = flip_pool.tile([P, CHUNK_TILES, P], F32, name="bank")
             for j in range(CHUNK_TILES):
                 nc.tensor.transpose(bank[:, j, :], product[:, c, j * P : (j + 1) * P], ident[:])
-            logs = run_pool.tile([P, CHUNK_TILES, P], F32, name="logs")
+            logs = run_pool.tile([P, CHUNK_TILES, P], F32, name="logs", align_bytes=256)
             nc.scalar.activation(out=logs[:], in_=bank[:], func=ACT.Ln)
             nc.vector.tensor_reduce(
                 out=logit_diff[:, c * CHUNK_TILES : (c + 1) * CHUNK_TILES], in_=logs[:],

@@ -20,20 +20,25 @@ WORDS = K_PASS // 2
 HID_TILES = HIDDEN // P
 BATCH_TILES = BATCH // P
 PAIR = 2 * P
+PAIR_TILES = 2
 PAIRS = BATCH // PAIR
 CHUNK_TILES = 4
 CHUNK = CHUNK_TILES * P
 CHUNKS = BATCH // CHUNK
 X_AHEAD = 6
-VECTOR_BANKS = 1
 TINY = 2.0 ** -30
+
+FIELD = 2.0 ** 23
+EXPONENT_BITS = 0x7F800000
+LOG2_E = 1.4426950408889634
+LN_2 = 0.6931471805599453
 
 FLOPS = 2 * BATCH * VISIBLE * HIDDEN
 
 
 def tile_rbm_kernel(tc, input_data, W_words, W_scales, U, h_bias, y_bias, out):
     nc = tc.nc
-    x_by_half = input_data.rearrange("(p c j) (h k) -> c h p j k", c=CHUNKS, j=CHUNK_TILES, h=2)
+    x_by_pair = input_data.rearrange("(p n j) k -> n p j k", n=PAIRS, j=PAIR_TILES)
 
     with ExitStack() as stack:
         const = stack.enter_context(tc.tile_pool(name="const", bufs=1))
@@ -41,8 +46,8 @@ def tile_rbm_kernel(tc, input_data, W_words, W_scales, U, h_bias, y_bias, out):
         mx_pool = stack.enter_context(tc.tile_pool(name="mx", bufs=3))
         on_pool = stack.enter_context(tc.tile_pool(name="on", bufs=2 * HID_TILES))
         run_pool = stack.enter_context(tc.tile_pool(name="run", bufs=2))
-        flip_pool = stack.enter_context(tc.psum_pool(name="flip", bufs=4))
-        acc_pool = stack.enter_context(tc.psum_pool(name="acc", bufs=HID_TILES))
+        flip_pool = stack.enter_context(tc.psum_pool(name="flip", bufs=6))
+        acc_pool = stack.enter_context(tc.psum_pool(name="acc", bufs=2))
         stack.enter_context(tc.manual_schedule())
 
         h_rows = const.tile([HID_TILES, P], BF16)
@@ -59,31 +64,38 @@ def tile_rbm_kernel(tc, input_data, W_words, W_scales, U, h_bias, y_bias, out):
         make_identity(nc, ident[:])
 
         x_pairs = {}
+        QUARTER_ORDER = [(j, h) for h in range(2) for j in range(2)]
 
-        def load_x(n, pieces=1):
+        def load_in_quarters(n):
+            x_pairs[n] = x_pool.tile([P, PAIR_TILES, VISIBLE], BF16, name="x_pair", align_bytes=256)
+            for j, h in QUARTER_ORDER:
+                k = slice(h * VISIBLE // 2, (h + 1) * VISIBLE // 2)
+                nc.sync.dma_start(out=x_pairs[n][:, j, k], in_=x_by_pair[n][:, j, k])
+
+        def load_x(n):
             if n < PAIRS:
-                x_pairs[n] = x_pool.tile([P, CHUNK_TILES, VISIBLE // 2], BF16, name="x_pair", align_bytes=256)
-                count = CHUNK_TILES // pieces
-                for i in range(pieces):
-                    rows = slice(i * count, (i + 1) * count)
-                    nc.sync.dma_start(out=x_pairs[n][:, rows, :], in_=x_by_half[n // 2][n % 2][:, rows, :])
+                x_pairs[n] = x_pool.tile([P, PAIR_TILES, VISIBLE], BF16, name="x_pair", align_bytes=256)
+                nc.sync.dma_start(out=x_pairs[n][:], in_=x_by_pair[n])
 
         w_codes = const.tile([P, PASSES, HIDDEN], U32, align_bytes=256)
-        load_x(0, pieces=2)
-        load_x(1, pieces=2)
         w_planes = const.tile([P, PASSES, HIDDEN], U8, align_bytes=256)
+        w_bytes = W_words.rearrange("g p n t -> p g (n t)").bitcast(I32)
+
+        def load_w(hidden):
+            nc.sync.dma_start(out=w_codes[:, :, hidden].bitcast(I32), in_=w_bytes[:, :, hidden])
+
+        load_in_quarters(0)
         nc.vector.memset(w_planes[:].bitcast(I32), 0)
+        load_w(slice(0, 2 * P))
         for quad in range(4):
             nc.sync.dma_start(
                 out=w_planes[32 * quad : 32 * quad + 4, :, :].bitcast(I32),
                 in_=W_scales[:, 4 * quad : 4 * quad + 4, :].rearrange("g r n -> r g n").bitcast(I32),
             )
-
-        nc.sync.dma_start(
-            out=w_codes[:].bitcast(I32),
-            in_=W_words.rearrange("g p n t -> p g (n t)").bitcast(I32),
-        )
-        for n in range(2, X_AHEAD):
+        load_w(slice(2 * P, 4 * P))
+        load_in_quarters(1)
+        load_in_quarters(2)
+        for n in range(3, X_AHEAD):
             load_x(n)
 
         as_rows = const.tile([P, 3, P], F32)
@@ -93,21 +105,38 @@ def tile_rbm_kernel(tc, input_data, W_words, W_scales, U, h_bias, y_bias, out):
         u_diff = const.tile([P, HID_TILES], F32)
         sig_pos = const.tile([P, HID_TILES], F32)
         sig_neg = const.tile([P, HID_TILES], F32)
+        inv_pos = const.tile([P, HID_TILES], F32)
         inv_neg = const.tile([P, HID_TILES], F32)
-        ratio = const.tile([P, HID_TILES], F32)
+        root = const.tile([P, HID_TILES], F32)
+        inv_root = const.tile([P, HID_TILES], F32)
         gain = const.tile([P, HID_TILES], F32)
         nudge = const.tile([P, HID_TILES], F32)
         factor = const.tile([P, HID_TILES], F32)
+        rise = const.tile([P, HID_TILES], F32)
         shift = const.tile([P, HID_TILES], F32)
         factor_pairs = const.tile([P, 2], F32)
         factor_all = const.tile([P, 1], F32)
-        y_diff = const.tile([P, 1], F32)
-        y_diff_neg = const.tile([P, 1], F32)
+        factor_shift = const.tile([P, 1], F32)
+        u_sum = const.tile([P, 1], F32)
+        u_total = const.tile([P, 1], F32)
+        y_raw = const.tile([P, 1], F32)
+        y_sum = const.tile([P, 1], F32)
+        log2_all = const.tile([P, 1], F32)
+        log2_int = const.tile([P, 1], I32)
+        log2_whole = const.tile([P, 1], F32)
+        log2_part = const.tile([P, 1], F32)
+        part_pos = const.tile([P, 1], F32)
+        part_neg = const.tile([P, 1], F32)
+        part_inv = const.tile([P, 1], F32)
+        field_bias = const.tile([P, 1], F32)
+        odds_scale = const.tile([P, 1], F32)
 
         def constants_onto_partitions():
             nc.vector.tensor_copy(out=as_rows[0:HID_TILES, 0, :], in_=h_rows[:])
             nc.vector.tensor_copy(out=as_rows[0:HID_TILES, 1:3, :], in_=u_rows[:].rearrange("t p c -> t c p"))
-            as_cols_ps = acc_pool.tile([P, 3, P], F32, name="acc")
+
+        def constants_transposed():
+            as_cols_ps = flip_pool.tile([P, 3, P], F32, name="bank")
             for m in range(3):
                 nc.tensor.transpose(as_cols_ps[:, m, :], as_rows[:, m, :], ident[:])
             return as_cols_ps
@@ -116,161 +145,316 @@ def tile_rbm_kernel(tc, input_data, W_words, W_scales, U, h_bias, y_bias, out):
             nc.vector.tensor_copy(out=as_cols[:], in_=as_cols_ps[:, :, 0:HID_TILES])
             nc.vector.tensor_add(out=sig_bias[:], in0=as_cols[:, 0, :], in1=as_cols[:, 2, :])
             nc.vector.tensor_sub(out=u_diff[:], in0=as_cols[:, 1, :], in1=as_cols[:, 2, :])
-            nc.scalar.activation(out=sig_pos[:], in_=u_diff[:], func=ACT.Sigmoid)
-            nc.scalar.activation(out=sig_neg[:], in_=u_diff[:], func=ACT.Sigmoid, scale=-1.0)
+            nc.scalar.activation(out=sig_pos[:], in_=u_diff[:], func=ACT.Sigmoid, scale=0.5)
+            nc.scalar.activation(out=sig_neg[:], in_=u_diff[:], func=ACT.Sigmoid, scale=-0.5)
 
-        def finish_constants():
-            nc.vector.reciprocal(out=inv_neg[:], in_=sig_neg[:])
-            nc.vector.tensor_mul(out=ratio[:], in0=sig_pos[:], in1=inv_neg[:])
-            nc.vector.tensor_scalar_add(out=gain[:], in0=ratio[:], scalar1=-1.0)
-            nc.vector.tensor_scalar(
+        def drip(steps, count=1):
+            for step in steps[:count]:
+                step()
+            for step in steps[:count]:
+                steps.remove(step)
+
+        gain_steps = [
+            lambda: nc.vector.reciprocal(out=inv_neg[:], in_=sig_neg[:]),
+            lambda: nc.vector.reciprocal(out=inv_pos[:], in_=sig_pos[:]),
+            lambda: nc.vector.tensor_mul(out=root[:], in0=sig_pos[:], in1=inv_neg[:]),
+            lambda: nc.vector.tensor_mul(out=inv_root[:], in0=sig_neg[:], in1=inv_pos[:]),
+            lambda: nc.vector.tensor_sub(out=gain[:], in0=root[:], in1=inv_root[:]),
+            lambda: nc.vector.tensor_scalar(
                 out=nudge[:], in0=gain[:], scalar1=0.0, scalar2=TINY, op0=ALU.is_equal, op1=ALU.mult
-            )
-            nc.vector.tensor_sub(out=y_diff[:], in0=y_all[:, 0:1], in1=y_all[:, 1:2])
-            nc.vector.tensor_add(out=factor[:], in0=gain[:], in1=nudge[:])
-            nc.vector.tensor_sub(out=y_diff_neg[:], in0=y_all[:, 1:2], in1=y_all[:, 0:1])
-            nc.vector.reciprocal(out=shift[:], in_=factor[:])
-            nc.vector.tensor_mul(out=factor_pairs[:], in0=factor[:, 0:2], in1=factor[:, 2:4])
-            nc.vector.tensor_mul(out=factor_all[:], in0=factor_pairs[:, 0:1], in1=factor_pairs[:, 1:2])
+            ),
+            lambda: nc.vector.tensor_add(out=factor[:], in0=gain[:], in1=nudge[:]),
+            lambda: nc.vector.tensor_mul(out=rise[:], in0=factor[:], in1=root[:]),
+            lambda: nc.vector.tensor_mul(out=factor_pairs[:], in0=factor[:, 0:2], in1=factor[:, 2:4]),
+            lambda: nc.vector.reciprocal(out=shift[:], in_=rise[:]),
+            lambda: nc.vector.tensor_mul(out=factor_all[:], in0=factor_pairs[:, 0:1], in1=factor_pairs[:, 1:2]),
+            lambda: nc.vector.tensor_mul(out=factor_shift[:], in0=factor_all[:], in1=shift[:, 0:1]),
+        ]
+        spread = {}
+
+        def spread_u_sum():
+            spread[0] = flip_pool.tile([P, P], F32, name="bank")
+            nc.tensor.transpose(spread[0][:], u_sum[:, 0:1].to_broadcast([P, P]), ident[:])
+
+        offset_steps = [
+            lambda: nc.vector.tensor_reduce(out=u_total[:], in_=spread[0][:], axis=mybir.AxisListType.X, op=ALU.add),
+            lambda: nc.vector.tensor_sub(out=y_raw[:], in0=y_all[:, 0:1], in1=y_all[:, 1:2]),
+            lambda: nc.vector.scalar_tensor_tensor(
+                out=y_sum[:], in0=u_total[:], scalar=0.5, in1=y_raw[:], op0=ALU.mult, op1=ALU.add
+            ),
+            lambda: nc.vector.tensor_scalar_mul(out=log2_all[:], in0=y_sum[:], scalar1=LOG2_E),
+            lambda: nc.vector.tensor_copy(out=log2_int[:], in_=log2_all[:]),
+            lambda: nc.vector.tensor_copy(out=log2_whole[:], in_=log2_int[:]),
+            lambda: nc.vector.tensor_sub(out=log2_part[:], in0=log2_all[:], in1=log2_whole[:]),
+            lambda: nc.vector.tensor_scalar(
+                out=field_bias[:], in0=log2_whole[:], scalar1=-FIELD, scalar2=-(32 * 127 + 48 - 127) * FIELD, op0=ALU.mult, op1=ALU.add
+            ),
+        ]
+
+        def offset_part():
+            nc.scalar.activation(out=part_pos[:], in_=log2_part[:], func=ACT.Sigmoid, scale=LN_2)
+            nc.scalar.activation(out=part_neg[:], in_=log2_part[:], func=ACT.Sigmoid, scale=-LN_2)
+
+        part_steps = [
+            lambda: nc.vector.reciprocal(out=part_inv[:], in_=part_pos[:]),
+            lambda: nc.vector.scalar_tensor_tensor(
+                out=odds_scale[:], in0=part_neg[:], scalar=2.0 ** 48, in1=part_inv[:], op0=ALU.mult, op1=ALU.mult
+            ),
+        ]
 
         sorted_x = {}
         grouped = {}
         codes = {}
         planes = {}
-        acc = {}
         on = {}
         running = {}
-        product = const.tile([P, CHUNKS, CHUNK], F32, align_bytes=256)
+        product = const.tile([P, BATCH], F32, align_bytes=256)
 
-        def sort_x(n, pieces=1):
-            if n < PAIRS:
-                sorted_x[n] = mx_pool.tile([P, 2 * PASSES, 2, P], F32, name="sorted_x", align_bytes=256)
-                words = (
-                    x_pairs[n][:].rearrange("b j k -> b (j k)").bitcast(F32).rearrange("b (s p u) -> b s u p", s=2 * PASSES, u=2)
-                )
-                count = 2 * PASSES // pieces
-                for i in range(pieces):
-                    part = slice(i * count, (i + 1) * count)
-                    nc.vector.tensor_copy(out=sorted_x[n][:, part], in_=words[:, part])
+        def words_of(n):
+            words = x_pairs[n][:].rearrange("b j k -> b (j k)").bitcast(F32)
+            return words.rearrange("b (s p u) -> b s u p", s=PAIR_TILES * PASSES, u=2)
 
-        def transpose_x(n):
+        def sort_tile(n):
+            sorted_x[n] = mx_pool.tile([P, PAIR_TILES * PASSES, 2, P], F32, name="sorted_x", align_bytes=256)
+
+        def sort_in_quarters(n):
+            sort_tile(n)
+            for j, h in QUARTER_ORDER:
+                part = slice(PASSES * j + 2 * h, PASSES * j + 2 * h + 2)
+                nc.vector.tensor_copy(out=sorted_x[n][:, part], in_=words_of(n)[:, part])
+                if n == 2:
+                    drip(gain_steps)
+
+        def sort_x(n):
             if n < PAIRS:
-                grouped[n] = mx_pool.tile([P, 2, 4 * CHUNK], BF16, name="grouped", align_bytes=256)
+                nc.vector.tensor_copy(out=sorted_x[n][:, scalar_share(n) :], in_=words_of(n)[:, scalar_share(n) :])
+
+        def scalar_share(n):
+            return 2 if n % 2 == 1 and n > 3 else 0
+
+        def sort_share(n):
+            if n < PAIRS:
+                sort_tile(n)
+                if scalar_share(n):
+                    nc.scalar.copy(out=sorted_x[n][:, : scalar_share(n)], in_=words_of(n)[:, : scalar_share(n)])
+
+        def transpose_x(n, vector_banks):
+            if n < PAIRS:
+                grouped[n] = mx_pool.tile([P, PASSES, 4 * PAIR], BF16, name="grouped", align_bytes=256)
                 dest = grouped[n][:].bitcast(F32).rearrange("p g (b u) -> p g b u", u=2)
-                for j in range(CHUNK_TILES):
+                for i in range(4):
+                    h, j = divmod(i, 2)
                     bank = flip_pool.tile([P, 2, 2, P], F32, name="bank")
                     for g in range(2):
                         for u in range(2):
-                            nc.tensor.transpose(bank[:, g, u, :], sorted_x[n][:, 2 * j + g, u, :], ident[:])
-                    if n % 2 == 1 and j < VECTOR_BANKS:
-                        nc.vector.tensor_copy(
-                            out=dest[:, :, j * P : (j + 1) * P, :],
-                            in_=bank[:].rearrange("p g u b -> p g b u"),
-                        )
+                            nc.tensor.transpose(bank[:, g, u, :], sorted_x[n][:, PASSES * j + 2 * h + g, u, :], ident[:])
+                    place = dest[:, 2 * h : 2 * h + 2, j * P : (j + 1) * P, :]
+                    if i in vector_banks:
+                        nc.vector.tensor_copy(out=place, in_=bank[:].rearrange("p g u b -> p g b u"))
                     else:
-                        nc.scalar.copy(
-                            out=dest[:, :, j * P : (j + 1) * P, :],
-                            in_=bank[:].rearrange("p g u b -> p g b u"),
-                        )
+                        nc.scalar.copy(out=place, in_=bank[:].rearrange("p g u b -> p g b u"))
 
-        def quantise(n):
+        def quantise(n, g0=0, g1=PASSES):
             if n < PAIRS:
-                codes[n] = mx_pool.tile([P, 2, CHUNK], U32, name="codes", align_bytes=256)
-                planes[n] = mx_pool.tile([P, 2, CHUNK], U8, name="planes", align_bytes=256)
+                if g0 == 0:
+                    codes[n] = mx_pool.tile([P, PASSES, PAIR], U32, name="codes", align_bytes=256)
+                    planes[n] = mx_pool.tile([P, PASSES, PAIR], U8, name="planes", align_bytes=256)
                 nc.vector.quantize_mx(
-                    out=codes[n][:].rearrange("p g b -> p (g b)").bitcast(FP8X4),
-                    scales=planes[n][:].rearrange("p g b -> p (g b)"),
-                    in_=grouped[n][:].rearrange("p g w -> p (g w)"),
+                    out=codes[n][:, g0:g1, :].rearrange("p g b -> p (g b)").bitcast(FP8X4),
+                    scales=planes[n][:, g0:g1, :].rearrange("p g b -> p (g b)"),
+                    in_=grouped[n][:, g0:g1, :].rearrange("p g w -> p (g w)"),
                 )
 
         def multiply(n):
             c, second = divmod(n, 2)
+            cols = slice(second * PAIR, (second + 1) * PAIR)
+            alone = n == PAIRS - 1
             for t in range(HID_TILES):
                 if not second:
-                    acc[(c, t)] = acc_pool.tile([P, CHUNK], F32, name="acc")
+                    on[(c, t)] = on_pool.tile([P, CHUNK], F32, name="on", align_bytes=256)
+                side = 0 if alone else t % 2
+                if alone:
+                    acc = flip_pool.tile([P, 1, PAIR], F32, name="bank")
+                elif side == 0:
+                    acc = acc_pool.tile([P, 2, PAIR], F32, name="acc")
                 hid = slice(t * P, (t + 1) * P)
-                for g in range(2):
+                for g in range(PASSES):
                     nc.tensor.matmul_mx(
-                        out=acc[(c, t)][:],
-                        lhsT=w_codes[:, 2 * second + g, hid].bitcast(FP8X4),
-                        lhsT_scale=w_planes[:, 2 * second + g, hid],
+                        out=acc[:, side, :],
+                        lhsT=w_codes[:, g, hid].bitcast(FP8X4),
+                        lhsT_scale=w_planes[:, g, hid],
                         rhs=codes[n][:, g, :].bitcast(FP8X4),
                         rhs_scale=planes[n][:, g, :],
-                        start=(not second and g == 0),
-                        stop=(second == 1 and g == 1),
+                        start=(g == 0),
+                        stop=(g == PASSES - 1),
                     )
-                if second:
-                    on[(c, t)] = on_pool.tile([P, CHUNK], F32, name="on", align_bytes=256)
-                    nc.scalar.activation(
-                        out=on[(c, t)][:], in_=acc[(c, t)][:], func=ACT.Sigmoid, bias=sig_bias[:, t : t + 1]
-                    )
+                if alone or side == 1:
+                    for i in range(side + 1):
+                        hidden = t - side + i
+                        nc.scalar.activation(
+                            out=on[(c, hidden)][:, cols], in_=acc[:, i, :], func=ACT.Sigmoid,
+                            bias=sig_bias[:, hidden : hidden + 1],
+                        )
+                    if t == 1:
+                        sort_share(n + 3)
+                    if c == CHUNKS - 1 and t == 1:
+                        extend_product(c, 0, cols)
 
-        def extend_product(c, t):
+        def extend_product(c, t, cols=slice(0, CHUNK)):
+            if t < HID_TILES - 1:
+                if (c, t) not in running:
+                    running[(c, t)] = run_pool.tile([P, CHUNK], F32, name="run%d" % t, align_bytes=256)
+                dest = running[(c, t)][:, cols]
+            else:
+                dest = product[:, c * CHUNK + cols.start : c * CHUNK + cols.stop]
             if t == 0:
-                running[(c, 0)] = run_pool.tile([P, CHUNK], F32, name="run0", align_bytes=256)
-                nc.vector.tensor_scalar(
-                    out=running[(c, 0)][:], in0=on[(c, 0)][:], scalar1=shift[:, 0:1], scalar2=factor_all[:, 0:1],
+                nc.scalar.activation(
+                    out=dest, in_=on[(c, 0)][:, cols], func=ACT.Identity, scale=factor_all[:, 0:1], bias=factor_shift[:, 0:1]
+                )
+            else:
+                nc.vector.scalar_tensor_tensor(
+                    out=dest, in0=on[(c, t)][:, cols], scalar=shift[:, t : t + 1], in1=running[(c, t - 1)][:, cols],
                     op0=ALU.add, op1=ALU.mult,
                 )
-                return
-            if t < HID_TILES - 1:
-                running[(c, t)] = run_pool.tile([P, CHUNK], F32, name="run%d" % t, align_bytes=256)
-                dest = running[(c, t)][:]
-            else:
-                dest = product[:, c, :]
-            nc.vector.scalar_tensor_tensor(
-                out=dest, in0=on[(c, t)][:], scalar=shift[:, t : t + 1], in1=running[(c, t - 1)][:],
-                op0=ALU.add, op1=ALU.mult,
-            )
 
-        sort_x(0, pieces=2)
-        transpose_x(0)
-        sort_x(1, pieces=2)
-        transpose_x(1)
-        columns = constants_onto_partitions()
-        quantise(0)
-        bias_and_difference(columns)
-        sort_x(2)
-        for c in range(CHUNKS):
-            load_x(2 * c + X_AHEAD)
-            load_x(2 * c + X_AHEAD + 1)
-            if c > 0:
-                extend_product(c - 1, 0)
-            quantise(2 * c + 1)
-            multiply(2 * c)
-            if c > 0:
-                extend_product(c - 1, 1)
-            sort_x(2 * c + 3)
-            if c > 0:
-                extend_product(c - 1, 2)
-            transpose_x(2 * c + 2)
-            quantise(2 * c + 2)
-            if c > 0:
-                extend_product(c - 1, 3)
-            sort_x(2 * c + 4)
-            if c == 0:
-                finish_constants()
-            multiply(2 * c + 1)
-            transpose_x(2 * c + 3)
-        for t in range(HID_TILES):
-            extend_product(CHUNKS - 1, t)
+        sixteens = const.tile([P, BATCH_TILES, P // 4], F32, align_bytes=256)
+        powers = const.tile([P, BATCH_TILES, P // 4], I32, align_bytes=256)
+        scaled = const.tile([P, BATCH_TILES, P // 4], F32, align_bytes=256)
+        mantissa = const.tile([P, BATCH_TILES], F32)
+        fields = const.tile([P, BATCH_TILES], F32)
+        back = {}
 
-        logit_diff = const.tile([P, BATCH_TILES], F32)
-        for c in range(CHUNKS):
-            bank = flip_pool.tile([P, CHUNK_TILES, P], F32, name="bank")
-            for j in range(CHUNK_TILES):
-                nc.tensor.transpose(bank[:, j, :], product[:, c, j * P : (j + 1) * P], ident[:])
-            logs = run_pool.tile([P, CHUNK_TILES, P], F32, name="logs", align_bytes=256)
-            nc.scalar.activation(out=logs[:], in_=bank[:], func=ACT.Ln)
+        def turn_back(first, count):
+            back[first] = flip_pool.tile([P, count, P], F32, name="bank")
+            for j in range(count):
+                nc.tensor.transpose(back[first][:, j, :], product[:, (first + j) * P : (first + j + 1) * P], ident[:])
+
+        def multiply_neighbours(first, count):
             nc.vector.tensor_reduce(
-                out=logit_diff[:, c * CHUNK_TILES : (c + 1) * CHUNK_TILES], in_=logs[:],
-                axis=mybir.AxisListType.X, op=ALU.add,
+                out=sixteens[:, first : first + count, :],
+                in_=back[first][:].rearrange("b j (q w) -> b j q w", w=4),
+                axis=mybir.AxisListType.X, op=ALU.mult,
             )
 
+        def find_powers(first, count):
+            tiles = slice(first, first + count)
+            nc.vector.tensor_scalar(
+                out=powers[:, tiles, :], in0=sixteens[:, tiles, :].bitcast(I32), scalar1=EXPONENT_BITS, scalar2=EXPONENT_BITS,
+                op0=ALU.bitwise_and, op1=ALU.bitwise_xor,
+            )
+
+        def scale_by_powers(first, count):
+            tiles = slice(first, first + count)
+            nc.vector.tensor_mul(out=scaled[:, tiles, :], in0=sixteens[:, tiles, :], in1=powers[:, tiles, :].bitcast(F32))
+
+        def reduce_fields(first, count):
+            tiles = slice(first, first + count)
+            nc.vector.tensor_reduce(out=fields[:, tiles], in_=powers[:, tiles, :], axis=mybir.AxisListType.X, op=ALU.add)
+
+        def reduce_mantissas(first, count):
+            tiles = slice(first, first + count)
+            nc.vector.tensor_reduce(out=mantissa[:, tiles], in_=scaled[:, tiles, :], axis=mybir.AxisListType.X, op=ALU.mult)
+
+        sort_in_quarters(0)
+        constants_onto_partitions()
+        transpose_x(0, (1, 3))
+        columns = constants_transposed()
+        quantise(0, 0, 2)
+        quantise(0, 2, 4)
+        bias_and_difference(columns)
+        sort_in_quarters(1)
+        nc.vector.tensor_reduce(out=u_sum[:], in_=u_diff[:], axis=mybir.AxisListType.X, op=ALU.add)
+        sort_in_quarters(2)
+        multiply(0)
+        transpose_x(1, (1, 3))
+        drip(gain_steps, 2)
+        quantise(1)
+        drip(gain_steps, 2)
+        load_x(X_AHEAD)
+        transpose_x(2, ())
+        sort_x(3)
+        drip(gain_steps, 2)
+        for n in range(1, PAIRS):
+            c, second = divmod(n, 2)
+            done = c - 1
+            load_x(n + X_AHEAD)
+            if done >= 0:
+                if second:
+                    extend_product(done, 3)
+                else:
+                    extend_product(done, 1)
+                    if n == PAIRS - 2:
+                        extend_product(done, 2)
+            quantise(n + 1)
+            if n == 1:
+                drip(gain_steps, 2)
+            if n > 2:
+                drip(offset_steps)
+            if n == 8:
+                drip(part_steps)
+            multiply(n)
+            if second and c < CHUNKS - 1:
+                extend_product(c, 0)
+            if n == 7:
+                offset_part()
+            if n >= 4 and not second:
+                multiply_neighbours(4 * (done - 1), 4)
+            if n == 11:
+                find_powers(0, 16)
+            if n == 12:
+                scale_by_powers(0, 16)
+            if n == 13:
+                reduce_fields(0, 16)
+                reduce_mantissas(0, 16)
+            sort_x(n + 3)
+            if n > 2:
+                drip(offset_steps)
+            if n == 8:
+                drip(part_steps)
+            if done >= 0 and not second and n < PAIRS - 2:
+                extend_product(done, 2)
+            transpose_x(n + 2, ())
+            if n == 2:
+                spread_u_sum()
+            if done >= 0 and second:
+                turn_back(4 * done, 4)
+        first, last = slice(0, PAIR), slice(PAIR, CHUNK)
+        for t in range(1, HID_TILES):
+            extend_product(CHUNKS - 1, t, first)
+        multiply_neighbours(24, 4)
+        turn_back(28, 2)
+        extend_product(CHUNKS - 1, 1, last)
+        multiply_neighbours(28, 2)
+        extend_product(CHUNKS - 1, 2, last)
+        find_powers(16, 14)
+        extend_product(CHUNKS - 1, 3, last)
+        turn_back(30, 2)
+        scale_by_powers(16, 14)
+        multiply_neighbours(30, 2)
+        reduce_fields(16, 14)
+        find_powers(30, 2)
+        reduce_mantissas(16, 14)
+        scale_by_powers(30, 2)
+        reduce_fields(30, 2)
+        reduce_mantissas(30, 2)
+
+        field_top = const.tile([P, BATCH_TILES], F32)
+        field_bits = const.tile([P, BATCH_TILES], I32)
+        total = const.tile([P, BATCH_TILES], F32)
+        inverse = const.tile([P, BATCH_TILES], F32)
         probs = const.tile([P, BATCH_TILES, 2], F32)
-        nc.scalar.activation(out=probs[:, :, 0], in_=logit_diff[:], func=ACT.Sigmoid, bias=y_diff[:, 0:1])
-        nc.scalar.activation(
-            out=probs[:, :, 1], in_=logit_diff[:], func=ACT.Sigmoid, bias=y_diff_neg[:, 0:1], scale=-1.0
+        nc.vector.tensor_scalar(
+            out=field_top[:], in0=fields[:], scalar1=field_bias[:, 0:1], scalar2=227 * FIELD, op0=ALU.add, op1=ALU.min
+        )
+        nc.vector.tensor_scalar_max(out=field_bits[:], in0=field_top[:], scalar1=27 * FIELD)
+        power = field_bits[:].bitcast(F32)
+        nc.vector.scalar_tensor_tensor(
+            out=total[:], in0=power, scalar=odds_scale[:, 0:1], in1=mantissa[:], op0=ALU.mult, op1=ALU.add
+        )
+        nc.vector.reciprocal(out=inverse[:], in_=total[:])
+        nc.vector.tensor_mul(out=probs[:, :, 0], in0=mantissa[:], in1=inverse[:])
+        nc.vector.scalar_tensor_tensor(
+            out=probs[:, :, 1], in0=power, scalar=odds_scale[:, 0:1], in1=inverse[:], op0=ALU.mult, op1=ALU.mult
         )
         nc.sync.dma_start(
             out=out.rearrange("(p i) c -> p (i c)", i=BATCH_TILES),

@@ -86,17 +86,21 @@ def tile_rbm_kernel(tc, input_data, W_words, W_scales, U, h_bias, y_bias, out):
 
         load_in_quarters(0)
         nc.vector.memset(w_planes[:].bitcast(I32), 0)
+        def load_scales():
+            for quad in range(4):
+                nc.sync.dma_start(
+                    out=w_planes[32 * quad : 32 * quad + 4, :, :].bitcast(I32),
+                    in_=W_scales[:, 4 * quad : 4 * quad + 4, :].rearrange("g r n -> r g n").bitcast(I32),
+                )
+
         load_w(slice(0, 2 * P))
-        for quad in range(4):
-            nc.sync.dma_start(
-                out=w_planes[32 * quad : 32 * quad + 4, :, :].bitcast(I32),
-                in_=W_scales[:, 4 * quad : 4 * quad + 4, :].rearrange("g r n -> r g n").bitcast(I32),
-            )
+        load_scales()
         load_w(slice(2 * P, 4 * P))
         load_in_quarters(1)
         load_in_quarters(2)
-        for n in range(3, X_AHEAD):
-            load_x(n)
+        load_x(3)
+        load_x(4)
+        load_x(5)
 
         as_rows = const.tile([P, 3, P], F32)
         nc.vector.memset(as_rows[:], 0.0)
@@ -222,23 +226,15 @@ def tile_rbm_kernel(tc, input_data, W_words, W_scales, U, h_bias, y_bias, out):
             for j, h in QUARTER_ORDER:
                 part = slice(PASSES * j + 2 * h, PASSES * j + 2 * h + 2)
                 nc.vector.tensor_copy(out=sorted_x[n][:, part], in_=words_of(n)[:, part])
-                if n == 2:
+                if n == 1:
                     drip(gain_steps)
 
         def sort_x(n):
             if n < PAIRS:
-                nc.vector.tensor_copy(out=sorted_x[n][:, scalar_share(n) :], in_=words_of(n)[:, scalar_share(n) :])
-
-        def scalar_share(n):
-            return 2 if n % 2 == 1 and n > 3 else 0
-
-        def sort_share(n):
-            if n < PAIRS:
                 sort_tile(n)
-                if scalar_share(n):
-                    nc.scalar.copy(out=sorted_x[n][:, : scalar_share(n)], in_=words_of(n)[:, : scalar_share(n)])
+                nc.vector.tensor_copy(out=sorted_x[n][:], in_=words_of(n))
 
-        def transpose_x(n, vector_banks):
+        def transpose_x(n, vector_banks, loose=False):
             if n < PAIRS:
                 grouped[n] = mx_pool.tile([P, PASSES, 4 * PAIR], BF16, name="grouped", align_bytes=256)
                 dest = grouped[n][:].bitcast(F32).rearrange("p g (b u) -> p g b u", u=2)
@@ -247,7 +243,7 @@ def tile_rbm_kernel(tc, input_data, W_words, W_scales, U, h_bias, y_bias, out):
                     bank = flip_pool.tile([P, 2, 2, P], F32, name="bank")
                     for g in range(2):
                         for u in range(2):
-                            nc.tensor.transpose(bank[:, g, u, :], sorted_x[n][:, PASSES * j + 2 * h + g, u, :], ident[:])
+                            nc.tensor.transpose(bank[:, g, u, :], (words_of(n) if loose else sorted_x[n])[:, PASSES * j + 2 * h + g, u, :], ident[:])
                     place = dest[:, 2 * h : 2 * h + 2, j * P : (j + 1) * P, :]
                     if i in vector_banks:
                         nc.vector.tensor_copy(out=place, in_=bank[:].rearrange("p g u b -> p g b u"))
@@ -295,21 +291,22 @@ def tile_rbm_kernel(tc, input_data, W_words, W_scales, U, h_bias, y_bias, out):
                             out=on[(c, hidden)][:, cols], in_=acc[:, i, :], func=ACT.Sigmoid,
                             bias=sig_bias[:, hidden : hidden + 1],
                         )
-                    if t == 1:
-                        sort_share(n + 3)
-                    if c == CHUNKS - 1 and t == 1:
-                        extend_product(c, 0, cols)
 
-        def extend_product(c, t, cols=slice(0, CHUNK)):
+        def extend_product(c, t, cols=slice(0, CHUNK), scalar=False):
             if t < HID_TILES - 1:
                 if (c, t) not in running:
                     running[(c, t)] = run_pool.tile([P, CHUNK], F32, name="run%d" % t, align_bytes=256)
                 dest = running[(c, t)][:, cols]
             else:
                 dest = product[:, c * CHUNK + cols.start : c * CHUNK + cols.stop]
-            if t == 0:
+            if t == 0 and scalar:
                 nc.scalar.activation(
                     out=dest, in_=on[(c, 0)][:, cols], func=ACT.Identity, scale=factor_all[:, 0:1], bias=factor_shift[:, 0:1]
+                )
+            elif t == 0:
+                nc.vector.tensor_scalar(
+                    out=dest, in0=on[(c, 0)][:, cols], scalar1=shift[:, 0:1], scalar2=factor_all[:, 0:1],
+                    op0=ALU.add, op1=ALU.mult,
                 )
             else:
                 nc.vector.scalar_tensor_tensor(
@@ -322,6 +319,7 @@ def tile_rbm_kernel(tc, input_data, W_words, W_scales, U, h_bias, y_bias, out):
         scaled = const.tile([P, BATCH_TILES, P // 4], F32, align_bytes=256)
         mantissa = const.tile([P, BATCH_TILES], F32)
         fields = const.tile([P, BATCH_TILES], F32)
+        field_copy = const.tile([P, BATCH_TILES, P // 4], F32, align_bytes=256)
         back = {}
 
         def turn_back(first, count):
@@ -351,89 +349,115 @@ def tile_rbm_kernel(tc, input_data, W_words, W_scales, U, h_bias, y_bias, out):
             tiles = slice(first, first + count)
             nc.vector.tensor_reduce(out=fields[:, tiles], in_=powers[:, tiles, :], axis=mybir.AxisListType.X, op=ALU.add)
 
+        def add_fields(first, count):
+            for tile in range(first, first + count):
+                nc.scalar.activation(
+                    out=field_copy[:, tile, :], in_=powers[:, tile, :].bitcast(U32), func=ACT.Copy, accum_out=fields[:, tile : tile + 1]
+                )
+
         def reduce_mantissas(first, count):
             tiles = slice(first, first + count)
             nc.vector.tensor_reduce(out=mantissa[:, tiles], in_=scaled[:, tiles, :], axis=mybir.AxisListType.X, op=ALU.mult)
 
-        sort_in_quarters(0)
         constants_onto_partitions()
-        transpose_x(0, (1, 3))
+        transpose_x(0, (1, 3), loose=True)
         columns = constants_transposed()
         quantise(0, 0, 2)
         quantise(0, 2, 4)
         bias_and_difference(columns)
         sort_in_quarters(1)
         nc.vector.tensor_reduce(out=u_sum[:], in_=u_diff[:], axis=mybir.AxisListType.X, op=ALU.add)
-        sort_in_quarters(2)
+        drip(gain_steps, 2)
         multiply(0)
         transpose_x(1, (1, 3))
-        drip(gain_steps, 2)
-        quantise(1)
-        drip(gain_steps, 2)
+        drip(gain_steps)
+        quantise(1, 0, 2)
+        drip(gain_steps)
+        quantise(1, 2, 4)
+        drip(gain_steps)
+        transpose_x(2, (), loose=True)
         load_x(X_AHEAD)
-        transpose_x(2, ())
         sort_x(3)
-        drip(gain_steps, 2)
-        for n in range(1, PAIRS):
+        drip(gain_steps)
+        for n in range(1, PAIRS - 3):
             c, second = divmod(n, 2)
             done = c - 1
             load_x(n + X_AHEAD)
             if done >= 0:
-                if second:
-                    extend_product(done, 3)
-                else:
-                    extend_product(done, 1)
-                    if n == PAIRS - 2:
-                        extend_product(done, 2)
+                extend_product(done, 2 * second)
             quantise(n + 1)
             if n == 1:
-                drip(gain_steps, 2)
+                drip(gain_steps)
             if n > 2:
                 drip(offset_steps)
             if n == 8:
                 drip(part_steps)
             multiply(n)
-            if second and c < CHUNKS - 1:
-                extend_product(c, 0)
             if n == 7:
                 offset_part()
-            if n >= 4 and not second:
-                multiply_neighbours(4 * (done - 1), 4)
-            if n == 11:
-                find_powers(0, 16)
-            if n == 12:
-                scale_by_powers(0, 16)
-            if n == 13:
-                reduce_fields(0, 16)
-                reduce_mantissas(0, 16)
+            if done >= 0:
+                extend_product(done, 2 * second + 1)
+            if n >= 8 and not second:
+                multiply_neighbours(4 * (n // 2 - 4), 4)
             sort_x(n + 3)
             if n > 2:
                 drip(offset_steps)
             if n == 8:
                 drip(part_steps)
-            if done >= 0 and not second and n < PAIRS - 2:
-                extend_product(done, 2)
             transpose_x(n + 2, ())
+            if n == 1:
+                drip(gain_steps)
             if n == 2:
                 spread_u_sum()
-            if done >= 0 and second:
-                turn_back(4 * done, 4)
+            if n >= 7 and second:
+                turn_back(4 * (c - 3), 4)
+            if n == 12:
+                turn_back(12, 4)
         first, last = slice(0, PAIR), slice(PAIR, CHUNK)
-        for t in range(1, HID_TILES):
-            extend_product(CHUNKS - 1, t, first)
+        extend_product(5, 2)
+        extend_product(5, 3)
+        quantise(14)
+        multiply_neighbours(12, 4)
+        find_powers(0, 16)
+        multiply(13)
+        scale_by_powers(0, 16)
+        transpose_x(15, ())
+        turn_back(16, 4)
+        extend_product(6, 0, slice(0, CHUNK), scalar=True)
+        quantise(15)
+        reduce_mantissas(0, 16)
+        multiply(14)
+        extend_product(7, 0, first, scalar=True)
+        add_fields(0, 16)
+        turn_back(20, 4)
+        multiply(15)
+        extend_product(7, 0, last, scalar=True)
+        extend_product(6, 1)
+        multiply_neighbours(16, 4)
+        extend_product(6, 2)
+        multiply_neighbours(20, 4)
+        extend_product(6, 3)
+        turn_back(24, 4)
+        extend_product(7, 1, first)
+        find_powers(16, 8)
+        add_fields(16, 8)
+        extend_product(7, 2, first)
         multiply_neighbours(24, 4)
+        extend_product(7, 3, first)
         turn_back(28, 2)
-        extend_product(CHUNKS - 1, 1, last)
+        scale_by_powers(16, 8)
+        extend_product(7, 1, last)
         multiply_neighbours(28, 2)
-        extend_product(CHUNKS - 1, 2, last)
-        find_powers(16, 14)
-        extend_product(CHUNKS - 1, 3, last)
+        extend_product(7, 2, last)
+        find_powers(24, 6)
+        add_fields(24, 6)
+        extend_product(7, 3, last)
         turn_back(30, 2)
-        scale_by_powers(16, 14)
+        reduce_mantissas(16, 8)
+        scale_by_powers(24, 6)
         multiply_neighbours(30, 2)
-        reduce_fields(16, 14)
+        reduce_mantissas(24, 6)
         find_powers(30, 2)
-        reduce_mantissas(16, 14)
         scale_by_powers(30, 2)
         reduce_fields(30, 2)
         reduce_mantissas(30, 2)

@@ -43,7 +43,7 @@ def tile_rbm_kernel(tc, input_data, W_words, W_scales, U, h_bias, y_bias, out):
     with ExitStack() as stack:
         const = stack.enter_context(tc.tile_pool(name="const", bufs=1))
         x_pool = stack.enter_context(tc.tile_pool(name="x", bufs=X_AHEAD))
-        mx_pool = stack.enter_context(tc.tile_pool(name="mx", bufs=3))
+        mx_pool = stack.enter_context(tc.tile_pool(name="mx", bufs=4))
         on_pool = stack.enter_context(tc.tile_pool(name="on", bufs=2 * HID_TILES))
         run_pool = stack.enter_context(tc.tile_pool(name="run", bufs=2))
         flip_pool = stack.enter_context(tc.psum_pool(name="flip", bufs=6))
@@ -261,7 +261,7 @@ def tile_rbm_kernel(tc, input_data, W_words, W_scales, U, h_bias, y_bias, out):
                     in_=grouped[n][:, g0:g1, :].rearrange("p g w -> p (g w)"),
                 )
 
-        def multiply(n):
+        def multiply(n, between=None):
             c, second = divmod(n, 2)
             cols = slice(second * PAIR, (second + 1) * PAIR)
             alone = n == PAIRS - 1
@@ -291,6 +291,8 @@ def tile_rbm_kernel(tc, input_data, W_words, W_scales, U, h_bias, y_bias, out):
                             out=on[(c, hidden)][:, cols], in_=acc[:, i, :], func=ACT.Sigmoid,
                             bias=sig_bias[:, hidden : hidden + 1],
                         )
+                    if t == 1 and between:
+                        between()
 
         def extend_product(c, t, cols=slice(0, CHUNK), scalar=False):
             if t < HID_TILES - 1:
@@ -385,6 +387,14 @@ def tile_rbm_kernel(tc, input_data, W_words, W_scales, U, h_bias, y_bias, out):
             load_x(n + X_AHEAD)
             if done >= 0:
                 extend_product(done, 2 * second)
+            if n >= 5 and second:
+                multiply_neighbours(4 * (c - 2), 4)
+            if n in (8, 12):
+                find_powers(2 * n - 16, 8)
+            if n == 9:
+                scale_by_powers(0, 8)
+            if n == 10:
+                reduce_mantissas(0, 8)
             quantise(n + 1)
             if n == 1:
                 drip(gain_steps)
@@ -397,63 +407,59 @@ def tile_rbm_kernel(tc, input_data, W_words, W_scales, U, h_bias, y_bias, out):
                 offset_part()
             if done >= 0:
                 extend_product(done, 2 * second + 1)
-            if n >= 8 and not second:
-                multiply_neighbours(4 * (n // 2 - 4), 4)
-            sort_x(n + 3)
+            if n == 10:
+                add_fields(0, 8)
+            if n == 1:
+                sort_x(4)
+            sort_x(n + 4)
             if n > 2:
                 drip(offset_steps)
             if n == 8:
                 drip(part_steps)
-            transpose_x(n + 2, ())
+            if n <= 2:
+                transpose_x(n + 2, ())
+            if n >= 2:
+                transpose_x(n + 3, ())
             if n == 1:
                 drip(gain_steps)
             if n == 2:
                 spread_u_sum()
-            if n >= 7 and second:
-                turn_back(4 * (c - 3), 4)
-            if n == 12:
-                turn_back(12, 4)
+            if n >= 4 and not second:
+                turn_back(4 * (c - 2), 4)
         first, last = slice(0, PAIR), slice(PAIR, CHUNK)
         extend_product(5, 2)
         extend_product(5, 3)
         quantise(14)
-        multiply_neighbours(12, 4)
-        find_powers(0, 16)
-        multiply(13)
-        scale_by_powers(0, 16)
-        transpose_x(15, ())
-        turn_back(16, 4)
-        extend_product(6, 0, slice(0, CHUNK), scalar=True)
-        quantise(15)
-        reduce_mantissas(0, 16)
-        multiply(14)
-        extend_product(7, 0, first, scalar=True)
-        add_fields(0, 16)
-        turn_back(20, 4)
-        multiply(15)
-        extend_product(7, 0, last, scalar=True)
-        extend_product(6, 1)
+        scale_by_powers(8, 8)
         multiply_neighbours(16, 4)
+        multiply(13, lambda: extend_product(6, 0, slice(0, CHUNK), scalar=True))
+        quantise(15)
+        extend_product(6, 1)
+        reduce_mantissas(8, 8)
+        multiply(14, lambda: extend_product(7, 0, first, scalar=True))
+        add_fields(8, 8)
         extend_product(6, 2)
-        multiply_neighbours(20, 4)
+        turn_back(20, 4)
+        multiply(15, lambda: extend_product(7, 0, last, scalar=True))
         extend_product(6, 3)
+        multiply_neighbours(20, 4)
         turn_back(24, 4)
         extend_product(7, 1, first)
         find_powers(16, 8)
         add_fields(16, 8)
         extend_product(7, 2, first)
-        multiply_neighbours(24, 4)
+        scale_by_powers(16, 8)
         extend_product(7, 3, first)
         turn_back(28, 2)
-        scale_by_powers(16, 8)
+        reduce_mantissas(16, 8)
         extend_product(7, 1, last)
-        multiply_neighbours(28, 2)
+        multiply_neighbours(24, 4)
         extend_product(7, 2, last)
-        find_powers(24, 6)
-        add_fields(24, 6)
+        multiply_neighbours(28, 2)
         extend_product(7, 3, last)
         turn_back(30, 2)
-        reduce_mantissas(16, 8)
+        find_powers(24, 6)
+        reduce_fields(24, 6)
         scale_by_powers(24, 6)
         multiply_neighbours(30, 2)
         reduce_mantissas(24, 6)

@@ -161,18 +161,18 @@ def tile_rbm_kernel(tc, input_data, W_words, W_scales, U, h_bias, y_bias, out):
         gain_steps = [
             lambda: nc.vector.reciprocal(out=inv_neg[:], in_=sig_neg[:]),
             lambda: nc.vector.reciprocal(out=inv_pos[:], in_=sig_pos[:]),
-            lambda: nc.vector.tensor_mul(out=root[:], in0=sig_pos[:], in1=inv_neg[:]),
-            lambda: nc.vector.tensor_mul(out=inv_root[:], in0=sig_neg[:], in1=inv_pos[:]),
-            lambda: nc.vector.tensor_sub(out=gain[:], in0=root[:], in1=inv_root[:]),
-            lambda: nc.vector.tensor_scalar(
+            lambda: nc.gpsimd.tensor_mul(out=root[:], in0=sig_pos[:], in1=inv_neg[:]),
+            lambda: nc.gpsimd.tensor_mul(out=inv_root[:], in0=sig_neg[:], in1=inv_pos[:]),
+            lambda: nc.gpsimd.tensor_sub(out=gain[:], in0=root[:], in1=inv_root[:]),
+            lambda: nc.gpsimd.tensor_scalar(
                 out=nudge[:], in0=gain[:], scalar1=0.0, scalar2=TINY, op0=ALU.is_equal, op1=ALU.mult
             ),
-            lambda: nc.vector.tensor_add(out=factor[:], in0=gain[:], in1=nudge[:]),
-            lambda: nc.vector.tensor_mul(out=rise[:], in0=factor[:], in1=root[:]),
-            lambda: nc.vector.tensor_mul(out=factor_pairs[:], in0=factor[:, 0:2], in1=factor[:, 2:4]),
+            lambda: nc.gpsimd.tensor_add(out=factor[:], in0=gain[:], in1=nudge[:]),
+            lambda: nc.gpsimd.tensor_mul(out=rise[:], in0=factor[:], in1=root[:]),
+            lambda: nc.gpsimd.tensor_mul(out=factor_pairs[:], in0=factor[:, 0:2], in1=factor[:, 2:4]),
             lambda: nc.vector.reciprocal(out=shift[:], in_=rise[:]),
-            lambda: nc.vector.tensor_mul(out=factor_all[:], in0=factor_pairs[:, 0:1], in1=factor_pairs[:, 1:2]),
-            lambda: nc.vector.tensor_mul(out=factor_shift[:], in0=factor_all[:], in1=shift[:, 0:1]),
+            lambda: nc.gpsimd.tensor_mul(out=factor_all[:], in0=factor_pairs[:, 0:1], in1=factor_pairs[:, 1:2]),
+            lambda: nc.gpsimd.tensor_mul(out=factor_shift[:], in0=factor_all[:], in1=shift[:, 0:1]),
         ]
         spread = {}
 
@@ -182,15 +182,15 @@ def tile_rbm_kernel(tc, input_data, W_words, W_scales, U, h_bias, y_bias, out):
 
         offset_steps = [
             lambda: nc.vector.tensor_reduce(out=u_total[:], in_=spread[0][:], axis=mybir.AxisListType.X, op=ALU.add),
-            lambda: nc.vector.tensor_sub(out=y_raw[:], in0=y_all[:, 0:1], in1=y_all[:, 1:2]),
-            lambda: nc.vector.scalar_tensor_tensor(
-                out=y_sum[:], in0=u_total[:], scalar=0.5, in1=y_raw[:], op0=ALU.mult, op1=ALU.add
+            lambda: nc.gpsimd.tensor_sub(out=y_raw[:], in0=y_all[:, 0:1], in1=y_all[:, 1:2]),
+            lambda: nc.gpsimd.tensor_scalar(
+                out=y_sum[:], in0=u_total[:], scalar1=0.5, scalar2=y_raw[:, 0:1], op0=ALU.mult, op1=ALU.add
             ),
-            lambda: nc.vector.tensor_scalar_mul(out=log2_all[:], in0=y_sum[:], scalar1=LOG2_E),
+            lambda: nc.gpsimd.tensor_scalar_mul(out=log2_all[:], in0=y_sum[:], scalar1=LOG2_E),
             lambda: nc.vector.tensor_copy(out=log2_int[:], in_=log2_all[:]),
             lambda: nc.vector.tensor_copy(out=log2_whole[:], in_=log2_int[:]),
-            lambda: nc.vector.tensor_sub(out=log2_part[:], in0=log2_all[:], in1=log2_whole[:]),
-            lambda: nc.vector.tensor_scalar(
+            lambda: nc.gpsimd.tensor_sub(out=log2_part[:], in0=log2_all[:], in1=log2_whole[:]),
+            lambda: nc.gpsimd.tensor_scalar(
                 out=field_bias[:], in0=log2_whole[:], scalar1=-FIELD, scalar2=-(32 * 127 + 48 - 127) * FIELD, op0=ALU.mult, op1=ALU.add
             ),
         ]
@@ -385,8 +385,9 @@ def tile_rbm_kernel(tc, input_data, W_words, W_scales, U, h_bias, y_bias, out):
             c, second = divmod(n, 2)
             done = c - 1
             load_x(n + X_AHEAD)
+            step = 2 * second + min(done, 1)
             if done >= 0:
-                extend_product(done, 2 * second)
+                extend_product(done, step)
             if n >= 5 and second:
                 multiply_neighbours(4 * (c - 2), 4)
             if n in (8, 12):
@@ -402,11 +403,11 @@ def tile_rbm_kernel(tc, input_data, W_words, W_scales, U, h_bias, y_bias, out):
                 drip(offset_steps)
             if n == 8:
                 drip(part_steps)
-            multiply(n)
+            multiply(n, (lambda chunk=c: extend_product(chunk, 0, scalar=True)) if second and c > 0 else None)
             if n == 7:
                 offset_part()
-            if done >= 0:
-                extend_product(done, 2 * second + 1)
+            if done >= 0 and step + 1 < HID_TILES:
+                extend_product(done, step + 1)
             if n == 10:
                 add_fields(0, 8)
             if n == 1:
@@ -427,31 +428,30 @@ def tile_rbm_kernel(tc, input_data, W_words, W_scales, U, h_bias, y_bias, out):
             if n >= 4 and not second:
                 turn_back(4 * (c - 2), 4)
         first, last = slice(0, PAIR), slice(PAIR, CHUNK)
-        extend_product(5, 2)
         extend_product(5, 3)
+        turn_back(20, 4)
         quantise(14)
         scale_by_powers(8, 8)
         multiply_neighbours(16, 4)
         multiply(13, lambda: extend_product(6, 0, slice(0, CHUNK), scalar=True))
         quantise(15)
+        multiply_neighbours(20, 4)
         extend_product(6, 1)
         reduce_mantissas(8, 8)
+        extend_product(6, 2)
+        find_powers(16, 8)
         multiply(14, lambda: extend_product(7, 0, first, scalar=True))
         add_fields(8, 8)
-        extend_product(6, 2)
-        turn_back(20, 4)
-        multiply(15, lambda: extend_product(7, 0, last, scalar=True))
         extend_product(6, 3)
-        multiply_neighbours(20, 4)
+        scale_by_powers(16, 8)
+        multiply(15, lambda: extend_product(7, 0, last, scalar=True))
         turn_back(24, 4)
         extend_product(7, 1, first)
-        find_powers(16, 8)
         add_fields(16, 8)
         extend_product(7, 2, first)
-        scale_by_powers(16, 8)
+        reduce_mantissas(16, 8)
         extend_product(7, 3, first)
         turn_back(28, 2)
-        reduce_mantissas(16, 8)
         extend_product(7, 1, last)
         multiply_neighbours(24, 4)
         extend_product(7, 2, last)
@@ -459,7 +459,8 @@ def tile_rbm_kernel(tc, input_data, W_words, W_scales, U, h_bias, y_bias, out):
         extend_product(7, 3, last)
         turn_back(30, 2)
         find_powers(24, 6)
-        reduce_fields(24, 6)
+        add_fields(24, 4)
+        reduce_fields(28, 2)
         scale_by_powers(24, 6)
         multiply_neighbours(30, 2)
         reduce_mantissas(24, 6)

@@ -30,7 +30,6 @@ TINY = 2.0 ** -30
 
 FIELD = 2.0 ** 23
 EXPONENT_BITS = 0x7F800000
-LOG2_E = 1.4426950408889634
 LN_2 = 0.6931471805599453
 
 FLOPS = 2 * BATCH * VISIBLE * HIDDEN
@@ -124,16 +123,8 @@ def tile_rbm_kernel(tc, input_data, W_words, W_scales, U, h_bias, y_bias, out):
         u_sum = const.tile([P, 1], F32)
         u_total = const.tile([P, 1], F32)
         y_raw = const.tile([P, 1], F32)
-        y_sum = const.tile([P, 1], F32)
-        log2_all = const.tile([P, 1], F32)
-        log2_int = const.tile([P, 1], I32)
-        log2_whole = const.tile([P, 1], F32)
-        log2_part = const.tile([P, 1], F32)
-        part_pos = const.tile([P, 1], F32)
-        part_neg = const.tile([P, 1], F32)
-        part_inv = const.tile([P, 1], F32)
-        field_bias = const.tile([P, 1], F32)
-        odds_scale = const.tile([P, 1], F32)
+        y_diff = const.tile([P, 1], F32)
+        y_diff_neg = const.tile([P, 1], F32)
 
         def constants_onto_partitions():
             nc.vector.tensor_copy(out=as_rows[0:HID_TILES, 0, :], in_=h_rows[:])
@@ -161,18 +152,18 @@ def tile_rbm_kernel(tc, input_data, W_words, W_scales, U, h_bias, y_bias, out):
         gain_steps = [
             lambda: nc.vector.reciprocal(out=inv_neg[:], in_=sig_neg[:]),
             lambda: nc.vector.reciprocal(out=inv_pos[:], in_=sig_pos[:]),
-            lambda: nc.gpsimd.tensor_mul(out=root[:], in0=sig_pos[:], in1=inv_neg[:]),
-            lambda: nc.gpsimd.tensor_mul(out=inv_root[:], in0=sig_neg[:], in1=inv_pos[:]),
-            lambda: nc.gpsimd.tensor_sub(out=gain[:], in0=root[:], in1=inv_root[:]),
-            lambda: nc.gpsimd.tensor_scalar(
+            lambda: nc.vector.tensor_mul(out=root[:], in0=sig_pos[:], in1=inv_neg[:]),
+            lambda: nc.vector.tensor_mul(out=inv_root[:], in0=sig_neg[:], in1=inv_pos[:]),
+            lambda: nc.vector.tensor_sub(out=gain[:], in0=root[:], in1=inv_root[:]),
+            lambda: nc.vector.tensor_scalar(
                 out=nudge[:], in0=gain[:], scalar1=0.0, scalar2=TINY, op0=ALU.is_equal, op1=ALU.mult
             ),
-            lambda: nc.gpsimd.tensor_add(out=factor[:], in0=gain[:], in1=nudge[:]),
-            lambda: nc.gpsimd.tensor_mul(out=rise[:], in0=factor[:], in1=root[:]),
-            lambda: nc.gpsimd.tensor_mul(out=factor_pairs[:], in0=factor[:, 0:2], in1=factor[:, 2:4]),
+            lambda: nc.vector.tensor_add(out=factor[:], in0=gain[:], in1=nudge[:]),
+            lambda: nc.vector.tensor_mul(out=rise[:], in0=factor[:], in1=root[:]),
+            lambda: nc.vector.tensor_mul(out=factor_pairs[:], in0=factor[:, 0:2], in1=factor[:, 2:4]),
             lambda: nc.vector.reciprocal(out=shift[:], in_=rise[:]),
-            lambda: nc.gpsimd.tensor_mul(out=factor_all[:], in0=factor_pairs[:, 0:1], in1=factor_pairs[:, 1:2]),
-            lambda: nc.gpsimd.tensor_mul(out=factor_shift[:], in0=factor_all[:], in1=shift[:, 0:1]),
+            lambda: nc.vector.tensor_mul(out=factor_all[:], in0=factor_pairs[:, 0:1], in1=factor_pairs[:, 1:2]),
+            lambda: nc.vector.tensor_mul(out=factor_shift[:], in0=factor_all[:], in1=shift[:, 0:1]),
         ]
         spread = {}
 
@@ -182,27 +173,12 @@ def tile_rbm_kernel(tc, input_data, W_words, W_scales, U, h_bias, y_bias, out):
 
         offset_steps = [
             lambda: nc.vector.tensor_reduce(out=u_total[:], in_=spread[0][:], axis=mybir.AxisListType.X, op=ALU.add),
-            lambda: nc.gpsimd.tensor_sub(out=y_raw[:], in0=y_all[:, 0:1], in1=y_all[:, 1:2]),
-            lambda: nc.gpsimd.tensor_scalar(
-                out=y_sum[:], in0=u_total[:], scalar1=0.5, scalar2=y_raw[:, 0:1], op0=ALU.mult, op1=ALU.add
+            lambda: nc.vector.tensor_sub(out=y_raw[:], in0=y_all[:, 0:1], in1=y_all[:, 1:2]),
+            lambda: nc.vector.tensor_scalar(
+                out=y_diff[:], in0=u_total[:], scalar1=0.5, scalar2=y_raw[:, 0:1], op0=ALU.mult, op1=ALU.add
             ),
-            lambda: nc.gpsimd.tensor_scalar_mul(out=log2_all[:], in0=y_sum[:], scalar1=LOG2_E),
-            lambda: nc.vector.tensor_copy(out=log2_int[:], in_=log2_all[:]),
-            lambda: nc.vector.tensor_copy(out=log2_whole[:], in_=log2_int[:]),
-            lambda: nc.gpsimd.tensor_sub(out=log2_part[:], in0=log2_all[:], in1=log2_whole[:]),
-            lambda: nc.gpsimd.tensor_scalar(
-                out=field_bias[:], in0=log2_whole[:], scalar1=-FIELD, scalar2=-(32 * 127 + 48 - 127) * FIELD, op0=ALU.mult, op1=ALU.add
-            ),
-        ]
-
-        def offset_part():
-            nc.scalar.activation(out=part_pos[:], in_=log2_part[:], func=ACT.Sigmoid, scale=LN_2)
-            nc.scalar.activation(out=part_neg[:], in_=log2_part[:], func=ACT.Sigmoid, scale=-LN_2)
-
-        part_steps = [
-            lambda: nc.vector.reciprocal(out=part_inv[:], in_=part_pos[:]),
-            lambda: nc.vector.scalar_tensor_tensor(
-                out=odds_scale[:], in0=part_neg[:], scalar=2.0 ** 48, in1=part_inv[:], op0=ALU.mult, op1=ALU.mult
+            lambda: nc.vector.tensor_scalar(
+                out=y_diff_neg[:], in0=y_diff[:], scalar1=-1.0, scalar2=0.0, op0=ALU.mult, op1=ALU.add
             ),
         ]
 
@@ -234,21 +210,34 @@ def tile_rbm_kernel(tc, input_data, W_words, W_scales, U, h_bias, y_bias, out):
                 sort_tile(n)
                 nc.vector.tensor_copy(out=sorted_x[n][:], in_=words_of(n))
 
-        def transpose_x(n, vector_banks, loose=False):
-            if n < PAIRS:
+        banks = {}
+
+        def flip_bank(n, i, loose=False):
+            if i == 0:
                 grouped[n] = mx_pool.tile([P, PASSES, 4 * PAIR], BF16, name="grouped", align_bytes=256)
-                dest = grouped[n][:].bitcast(F32).rearrange("p g (b u) -> p g b u", u=2)
-                for i in range(4):
-                    h, j = divmod(i, 2)
-                    bank = flip_pool.tile([P, 2, 2, P], F32, name="bank")
-                    for g in range(2):
-                        for u in range(2):
-                            nc.tensor.transpose(bank[:, g, u, :], (words_of(n) if loose else sorted_x[n])[:, PASSES * j + 2 * h + g, u, :], ident[:])
-                    place = dest[:, 2 * h : 2 * h + 2, j * P : (j + 1) * P, :]
-                    if i in vector_banks:
-                        nc.vector.tensor_copy(out=place, in_=bank[:].rearrange("p g u b -> p g b u"))
-                    else:
-                        nc.scalar.copy(out=place, in_=bank[:].rearrange("p g u b -> p g b u"))
+            h, j = divmod(i, 2)
+            bank = flip_pool.tile([P, 2, 2, P], F32, name="bank")
+            banks[(n, i)] = bank
+            for g in range(2):
+                for u in range(2):
+                    nc.tensor.transpose(bank[:, g, u, :], (words_of(n) if loose else sorted_x[n])[:, PASSES * j + 2 * h + g, u, :], ident[:])
+
+        def empty_bank(n, i, vector):
+            h, j = divmod(i, 2)
+            dest = grouped[n][:].bitcast(F32).rearrange("p g (b u) -> p g b u", u=2)
+            place = dest[:, 2 * h : 2 * h + 2, j * P : (j + 1) * P, :]
+            if vector:
+                nc.vector.tensor_copy(out=place, in_=banks[(n, i)][:].rearrange("p g u b -> p g b u"))
+            else:
+                nc.scalar.copy(out=place, in_=banks[(n, i)][:].rearrange("p g u b -> p g b u"))
+
+        def transpose_x(n, loose=False):
+            for i in range(4):
+                flip_bank(n, i, loose)
+
+        def empty_banks(n, engines="ssss"):
+            for i in range(4):
+                empty_bank(n, i, engines[i] == "v")
 
         def quantise(n, g0=0, g1=PASSES):
             if n < PAIRS:
@@ -361,23 +350,55 @@ def tile_rbm_kernel(tc, input_data, W_words, W_scales, U, h_bias, y_bias, out):
             tiles = slice(first, first + count)
             nc.vector.tensor_reduce(out=mantissa[:, tiles], in_=scaled[:, tiles, :], axis=mybir.AxisListType.X, op=ALU.mult)
 
+        logit_diff = const.tile([P, BATCH_TILES], F32)
+        rest_logs = const.tile([P, BATCH_TILES], F32)
+        power_logs = const.tile([P, BATCH_TILES], F32)
+        logs = {}
+
+        def log_rests(first, count):
+            nc.scalar.activation(out=rest_logs[:, first : first + count], in_=mantissa[:, first : first + count], func=ACT.Ln, scale=2.0 ** -48)
+
+        def log_powers(first, count):
+            nc.vector.tensor_scalar(
+                out=power_logs[:, first : first + count], in0=fields[:, first : first + count],
+                scalar1=-(32 * 127 + 48) * FIELD, scalar2=-LN_2 / FIELD, op0=ALU.add, op1=ALU.mult,
+            )
+
+        def add_logs(first, count):
+            tiles = slice(first, first + count)
+            nc.vector.tensor_add(out=logit_diff[:, tiles], in0=rest_logs[:, tiles], in1=power_logs[:, tiles])
+
+        def log_products(first, count):
+            logs[first] = run_pool.tile([P, count, P], F32, name="logs%d" % count, align_bytes=256)
+            nc.scalar.activation(out=logs[first][:], in_=back[first][:], func=ACT.Ln)
+
+        def sum_logs(first, count):
+            nc.vector.tensor_reduce(
+                out=logit_diff[:, first : first + count], in_=logs[first][:], axis=mybir.AxisListType.X, op=ALU.add
+            )
+
         constants_onto_partitions()
-        transpose_x(0, (1, 3), loose=True)
-        columns = constants_transposed()
+        transpose_x(0, loose=True)
+        empty_bank(0, 0, False)
+        empty_bank(0, 1, True)
         quantise(0, 0, 2)
+        empty_bank(0, 2, False)
+        empty_bank(0, 3, False)
+        columns = constants_transposed()
         quantise(0, 2, 4)
         bias_and_difference(columns)
         sort_in_quarters(1)
         nc.vector.tensor_reduce(out=u_sum[:], in_=u_diff[:], axis=mybir.AxisListType.X, op=ALU.add)
-        drip(gain_steps, 2)
-        multiply(0)
-        transpose_x(1, (1, 3))
         drip(gain_steps)
+        multiply(0)
+        transpose_x(1)
+        empty_banks(1, "svsv")
         quantise(1, 0, 2)
         drip(gain_steps)
         quantise(1, 2, 4)
-        drip(gain_steps)
-        transpose_x(2, (), loose=True)
+        drip(gain_steps, 2)
+        transpose_x(2, loose=True)
+        empty_banks(2)
         load_x(X_AHEAD)
         sort_x(3)
         drip(gain_steps)
@@ -401,26 +422,21 @@ def tile_rbm_kernel(tc, input_data, W_words, W_scales, U, h_bias, y_bias, out):
                 drip(gain_steps)
             if n > 2:
                 drip(offset_steps)
-            if n == 8:
-                drip(part_steps)
             multiply(n, (lambda chunk=c: extend_product(chunk, 0, scalar=True)) if second and c > 0 else None)
-            if n == 7:
-                offset_part()
             if done >= 0 and step + 1 < HID_TILES:
                 extend_product(done, step + 1)
             if n == 10:
                 add_fields(0, 8)
             if n == 1:
                 sort_x(4)
+                drip(gain_steps)
             sort_x(n + 4)
             if n > 2:
                 drip(offset_steps)
-            if n == 8:
-                drip(part_steps)
-            if n <= 2:
-                transpose_x(n + 2, ())
-            if n >= 2:
-                transpose_x(n + 3, ())
+            ahead = (n + 2,) if n == 1 else (n + 2, n + 3) if n == 2 else (n + 3,)
+            for m in ahead:
+                transpose_x(m)
+                empty_banks(m)
             if n == 1:
                 drip(gain_steps)
             if n == 2:
@@ -432,6 +448,7 @@ def tile_rbm_kernel(tc, input_data, W_words, W_scales, U, h_bias, y_bias, out):
         turn_back(20, 4)
         quantise(14)
         scale_by_powers(8, 8)
+        add_fields(8, 8)
         multiply_neighbours(16, 4)
         multiply(13, lambda: extend_product(6, 0, slice(0, CHUNK), scalar=True))
         quantise(15)
@@ -441,51 +458,34 @@ def tile_rbm_kernel(tc, input_data, W_words, W_scales, U, h_bias, y_bias, out):
         extend_product(6, 2)
         find_powers(16, 8)
         multiply(14, lambda: extend_product(7, 0, first, scalar=True))
-        add_fields(8, 8)
+        add_fields(16, 8)
         extend_product(6, 3)
         scale_by_powers(16, 8)
         multiply(15, lambda: extend_product(7, 0, last, scalar=True))
         turn_back(24, 4)
         extend_product(7, 1, first)
-        add_fields(16, 8)
-        extend_product(7, 2, first)
         reduce_mantissas(16, 8)
+        extend_product(7, 2, first)
+        extend_product(7, 1, last)
         extend_product(7, 3, first)
         turn_back(28, 2)
-        extend_product(7, 1, last)
-        multiply_neighbours(24, 4)
         extend_product(7, 2, last)
-        multiply_neighbours(28, 2)
+        log_powers(0, 24)
         extend_product(7, 3, last)
         turn_back(30, 2)
-        find_powers(24, 6)
-        add_fields(24, 4)
-        reduce_fields(28, 2)
-        scale_by_powers(24, 6)
-        multiply_neighbours(30, 2)
-        reduce_mantissas(24, 6)
-        find_powers(30, 2)
-        scale_by_powers(30, 2)
-        reduce_fields(30, 2)
-        reduce_mantissas(30, 2)
+        log_rests(0, 24)
+        log_products(24, 4)
+        log_products(28, 2)
+        log_products(30, 2)
+        add_logs(0, 24)
+        sum_logs(24, 4)
+        sum_logs(28, 2)
+        sum_logs(30, 2)
 
-        field_top = const.tile([P, BATCH_TILES], F32)
-        field_bits = const.tile([P, BATCH_TILES], I32)
-        total = const.tile([P, BATCH_TILES], F32)
-        inverse = const.tile([P, BATCH_TILES], F32)
         probs = const.tile([P, BATCH_TILES, 2], F32)
-        nc.vector.tensor_scalar(
-            out=field_top[:], in0=fields[:], scalar1=field_bias[:, 0:1], scalar2=227 * FIELD, op0=ALU.add, op1=ALU.min
-        )
-        nc.vector.tensor_scalar_max(out=field_bits[:], in0=field_top[:], scalar1=27 * FIELD)
-        power = field_bits[:].bitcast(F32)
-        nc.vector.scalar_tensor_tensor(
-            out=total[:], in0=power, scalar=odds_scale[:, 0:1], in1=mantissa[:], op0=ALU.mult, op1=ALU.add
-        )
-        nc.vector.reciprocal(out=inverse[:], in_=total[:])
-        nc.vector.tensor_mul(out=probs[:, :, 0], in0=mantissa[:], in1=inverse[:])
-        nc.vector.scalar_tensor_tensor(
-            out=probs[:, :, 1], in0=power, scalar=odds_scale[:, 0:1], in1=inverse[:], op0=ALU.mult, op1=ALU.mult
+        nc.scalar.activation(out=probs[:, :, 0], in_=logit_diff[:], func=ACT.Sigmoid, bias=y_diff[:, 0:1])
+        nc.scalar.activation(
+            out=probs[:, :, 1], in_=logit_diff[:], func=ACT.Sigmoid, bias=y_diff_neg[:, 0:1], scale=-1.0
         )
         nc.sync.dma_start(
             out=out.rearrange("(p i) c -> p (i c)", i=BATCH_TILES),

@@ -25,6 +25,7 @@ PAIRS = BATCH // PAIR
 CHUNK_TILES = 4
 CHUNK = CHUNK_TILES * P
 CHUNKS = BATCH // CHUNK
+DEEPER = 5
 X_AHEAD = 6
 TINY = 2.0 ** -30
 
@@ -310,7 +311,6 @@ def tile_rbm_kernel(tc, input_data, W_words, W_scales, U, h_bias, y_bias, out):
         scaled = const.tile([P, BATCH_TILES, P // 4], F32, align_bytes=256)
         mantissa = const.tile([P, BATCH_TILES], F32)
         fields = const.tile([P, BATCH_TILES], F32)
-        field_copy = const.tile([P, BATCH_TILES, P // 4], F32, align_bytes=256)
         back = {}
 
         def turn_back(first, count):
@@ -339,12 +339,6 @@ def tile_rbm_kernel(tc, input_data, W_words, W_scales, U, h_bias, y_bias, out):
         def reduce_fields(first, count):
             tiles = slice(first, first + count)
             nc.vector.tensor_reduce(out=fields[:, tiles], in_=powers[:, tiles, :], axis=mybir.AxisListType.X, op=ALU.add)
-
-        def add_fields(first, count):
-            for tile in range(first, first + count):
-                nc.scalar.activation(
-                    out=field_copy[:, tile, :], in_=powers[:, tile, :].bitcast(U32), func=ACT.Copy, accum_out=fields[:, tile : tile + 1]
-                )
 
         def reduce_mantissas(first, count):
             tiles = slice(first, first + count)
@@ -426,15 +420,16 @@ def tile_rbm_kernel(tc, input_data, W_words, W_scales, U, h_bias, y_bias, out):
             if done >= 0 and step + 1 < HID_TILES:
                 extend_product(done, step + 1)
             if n == 10:
-                add_fields(0, 8)
+                reduce_fields(0, 8)
+            if n < DEEPER:
+                sort_x(n + 3)
+            if n >= DEEPER - 1:
+                sort_x(n + 4)
             if n == 1:
-                sort_x(4)
                 drip(gain_steps)
-            sort_x(n + 4)
             if n > 2:
                 drip(offset_steps)
-            ahead = (n + 2,) if n == 1 else (n + 2, n + 3) if n == 2 else (n + 3,)
-            for m in ahead:
+            for m in range(n + 2 if n <= DEEPER else n + 3, n + 3 if n < DEEPER else n + 4):
                 transpose_x(m)
                 empty_banks(m)
             if n == 1:
@@ -448,7 +443,7 @@ def tile_rbm_kernel(tc, input_data, W_words, W_scales, U, h_bias, y_bias, out):
         turn_back(20, 4)
         quantise(14)
         scale_by_powers(8, 8)
-        add_fields(8, 8)
+        reduce_fields(8, 8)
         multiply_neighbours(16, 4)
         multiply(13, lambda: extend_product(6, 0, slice(0, CHUNK), scalar=True))
         quantise(15)
@@ -458,7 +453,7 @@ def tile_rbm_kernel(tc, input_data, W_words, W_scales, U, h_bias, y_bias, out):
         extend_product(6, 2)
         find_powers(16, 8)
         multiply(14, lambda: extend_product(7, 0, first, scalar=True))
-        add_fields(16, 8)
+        reduce_fields(16, 8)
         extend_product(6, 3)
         scale_by_powers(16, 8)
         multiply(15, lambda: extend_product(7, 0, last, scalar=True))

@@ -81,8 +81,8 @@ def tile_rbm_kernel(tc, input_data, W_words, W_scales, U, h_bias, y_bias, out):
         w_planes = const.tile([P, PASSES, HIDDEN], U8, align_bytes=256)
         w_bytes = W_words.rearrange("g p n t -> p g (n t)").bitcast(I32)
 
-        def load_w(hidden):
-            nc.sync.dma_start(out=w_codes[:, :, hidden].bitcast(I32), in_=w_bytes[:, :, hidden])
+        def load_w(passes):
+            nc.sync.dma_start(out=w_codes[:, passes, :].bitcast(I32), in_=w_bytes[:, passes, :])
 
         load_in_quarters(0)
         nc.vector.memset(w_planes[:].bitcast(I32), 0)
@@ -93,9 +93,9 @@ def tile_rbm_kernel(tc, input_data, W_words, W_scales, U, h_bias, y_bias, out):
                     in_=W_scales[:, 4 * quad : 4 * quad + 4, :].rearrange("g r n -> r g n").bitcast(I32),
                 )
 
-        load_w(slice(0, 2 * P))
+        load_w(slice(0, 2))
         load_scales()
-        load_w(slice(2 * P, 4 * P))
+        load_w(slice(2, 4))
         load_in_quarters(1)
         load_in_quarters(2)
         load_x(3)
@@ -366,6 +366,19 @@ def tile_rbm_kernel(tc, input_data, W_words, W_scales, U, h_bias, y_bias, out):
             logs[first] = run_pool.tile([P, count, P], F32, name="logs%d" % count, align_bytes=256)
             nc.scalar.activation(out=logs[first][:], in_=back[first][:], func=ACT.Ln)
 
+        twos = {}
+
+        def multiply_pairs(first, count):
+            twos[first] = run_pool.tile([P, count, P // 2], F32, name="twos", align_bytes=256)
+            nc.vector.tensor_reduce(
+                out=twos[first][:], in_=back[first][:].rearrange("b j (q w) -> b j q w", w=2),
+                axis=mybir.AxisListType.X, op=ALU.mult,
+            )
+
+        def log_pairs(first, count):
+            logs[first] = run_pool.tile([P, count, P // 2], F32, name="logs_of_twos", align_bytes=256)
+            nc.scalar.activation(out=logs[first][:], in_=twos[first][:], func=ACT.Ln)
+
         def sum_logs(first, count):
             nc.vector.tensor_reduce(
                 out=logit_diff[:, first : first + count], in_=logs[first][:], axis=mybir.AxisListType.X, op=ALU.add
@@ -468,14 +481,16 @@ def tile_rbm_kernel(tc, input_data, W_words, W_scales, U, h_bias, y_bias, out):
         log_powers(0, 24)
         extend_product(7, 3, last)
         turn_back(30, 2)
+        multiply_pairs(24, 4)
+        multiply_pairs(28, 2)
         log_rests(0, 24)
-        log_products(24, 4)
-        log_products(28, 2)
         log_products(30, 2)
+        log_pairs(24, 4)
+        log_pairs(28, 2)
         add_logs(0, 24)
+        sum_logs(30, 2)
         sum_logs(24, 4)
         sum_logs(28, 2)
-        sum_logs(30, 2)
 
         probs = const.tile([P, BATCH_TILES, 2], F32)
         nc.scalar.activation(out=probs[:, :, 0], in_=logit_diff[:], func=ACT.Sigmoid, bias=y_diff[:, 0:1])

from contextlib import ExitStack

import concourse.mybir as mybir
from concourse.masks import make_identity

F32 = mybir.dt.float32
BF16 = mybir.dt.bfloat16
I32 = mybir.dt.int32
U32 = mybir.dt.uint32
U8 = mybir.dt.uint8
FP8X4 = mybir.dt.float8_e4m3fn_x4
ACT = mybir.ActivationFunctionType
ALU = mybir.AluOpType

P = 128
BATCH, VISIBLE, HIDDEN = 4096, 2048, 512
K_PASS = 4 * P
PASSES = VISIBLE // K_PASS
WORDS = K_PASS // 2
HID_TILES = HIDDEN // P
BATCH_TILES = BATCH // P
PAIR = 2 * P
PAIR_TILES = 2
PAIRS = BATCH // PAIR
CHUNK_TILES = 4
CHUNK = CHUNK_TILES * P
CHUNKS = BATCH // CHUNK
DEEPER = 5
X_AHEAD = 6
TINY = 2.0 ** -30

FIELD = 2.0 ** 23
EXPONENT_BITS = 0x7F800000
LN_2 = 0.6931471805599453

FLOPS = 2 * BATCH * VISIBLE * HIDDEN


def tile_rbm_kernel(tc, input_data, W_words, W_scales, U, h_bias, y_bias, out):
    nc = tc.nc
    x_by_pair = input_data.rearrange("(p n j) k -> n p j k", n=PAIRS, j=PAIR_TILES)

    with ExitStack() as stack:
        const = stack.enter_context(tc.tile_pool(name="const", bufs=1))
        x_pool = stack.enter_context(tc.tile_pool(name="x", bufs=X_AHEAD))
        mx_pool = stack.enter_context(tc.tile_pool(name="mx", bufs=4))
        on_pool = stack.enter_context(tc.tile_pool(name="on", bufs=2 * HID_TILES))
        run_pool = stack.enter_context(tc.tile_pool(name="run", bufs=2))
        flip_pool = stack.enter_context(tc.psum_pool(name="flip", bufs=6))
        acc_pool = stack.enter_context(tc.psum_pool(name="acc", bufs=2))
        stack.enter_context(tc.manual_schedule())

        h_rows = const.tile([HID_TILES, P], BF16)
        u_rows = const.tile([HID_TILES, P, 2], BF16)
        y_all = const.tile([P, 2], BF16)
        nc.scalar.dma_start(out=h_rows[:], in_=h_bias.rearrange("o (t p) -> (o t) p", p=P))
        nc.scalar.dma_start(out=u_rows[:], in_=U.rearrange("(t p) c -> t p c", p=P))
        nc.scalar.dma_start(out=y_all[:], in_=y_bias.rearrange("o c -> (o c)").partition_broadcast(P))
        warm = const.tile([P, 2], F32)
        nc.vector.memset(warm[:, 0:1], 0.0)
        nc.scalar.activation(out=warm[:, 1:2], in_=warm[:, 0:1], func=ACT.Sigmoid)

        ident = const.tile([P, P], F32, align_bytes=256)
        make_identity(nc, ident[:])

        x_pairs = {}
        QUARTER_ORDER = [(j, h) for h in range(2) for j in range(2)]

        def load_in_quarters(n):
            x_pairs[n] = x_pool.tile([P, PAIR_TILES, VISIBLE], BF16, name="x_pair", align_bytes=256)
            for j, h in QUARTER_ORDER:
                k = slice(h * VISIBLE // 2, (h + 1) * VISIBLE // 2)
                nc.sync.dma_start(out=x_pairs[n][:, j, k], in_=x_by_pair[n][:, j, k])

        def load_x(n):
            if n < PAIRS:
                x_pairs[n] = x_pool.tile([P, PAIR_TILES, VISIBLE], BF16, name="x_pair", align_bytes=256)
                nc.sync.dma_start(out=x_pairs[n][:], in_=x_by_pair[n])

        w_codes = const.tile([P, PASSES, HIDDEN], U32, align_bytes=256)
        w_planes = const.tile([P, PASSES, HIDDEN], U8, align_bytes=256)
        w_bytes = W_words.rearrange("g p n t -> p g (n t)").bitcast(I32)

        def load_w(passes):
            nc.sync.dma_start(out=w_codes[:, passes, :].bitcast(I32), in_=w_bytes[:, passes, :])

        load_in_quarters(0)
        nc.vector.memset(w_planes[:].bitcast(I32), 0)
        def load_scales():
            for quad in range(4):
                nc.sync.dma_start(
                    out=w_planes[32 * quad : 32 * quad + 4, :, :].bitcast(I32),
                    in_=W_scales[:, 4 * quad : 4 * quad + 4, :].rearrange("g r n -> r g n").bitcast(I32),
                )

        load_w(slice(0, 2))
        load_scales()
        load_w(slice(2, 4))
        load_in_quarters(1)
        load_in_quarters(2)
        load_x(3)
        load_x(4)
        load_x(5)

        as_rows = const.tile([P, 3, P], F32)
        nc.vector.memset(as_rows[:], 0.0)
        as_cols = const.tile([P, 3, HID_TILES], F32)
        sig_bias = const.tile([P, HID_TILES], F32)
        u_diff = const.tile([P, HID_TILES], F32)
        sig_pos = const.tile([P, HID_TILES], F32)
        sig_neg = const.tile([P, HID_TILES], F32)
        inv_pos = const.tile([P, HID_TILES], F32)
        inv_neg = const.tile([P, HID_TILES], F32)
        root = const.tile([P, HID_TILES], F32)
        inv_root = const.tile([P, HID_TILES], F32)
        gain = const.tile([P, HID_TILES], F32)
        nudge = const.tile([P, HID_TILES], F32)
        factor = const.tile([P, HID_TILES], F32)
        rise = const.tile([P, HID_TILES], F32)
        shift = const.tile([P, HID_TILES], F32)
        factor_pairs = const.tile([P, 2], F32)
        factor_all = const.tile([P, 1], F32)
        factor_shift = const.tile([P, 1], F32)
        u_sum = const.tile([P, 1], F32)
        u_total = const.tile([P, 1], F32)
        y_raw = const.tile([P, 1], F32)
        y_diff = const.tile([P, 1], F32)
        y_diff_neg = const.tile([P, 1], F32)

        def constants_onto_partitions():
            nc.vector.tensor_copy(out=as_rows[0:HID_TILES, 0, :], in_=h_rows[:])
            nc.vector.tensor_copy(out=as_rows[0:HID_TILES, 1:3, :], in_=u_rows[:].rearrange("t p c -> t c p"))

        def constants_transposed():
            as_cols_ps = flip_pool.tile([P, 3, P], F32, name="bank")
            for m in range(3):
                nc.tensor.transpose(as_cols_ps[:, m, :], as_rows[:, m, :], ident[:])
            return as_cols_ps

        def bias_and_difference(as_cols_ps):
            nc.vector.tensor_copy(out=as_cols[:], in_=as_cols_ps[:, :, 0:HID_TILES])
            nc.vector.tensor_add(out=sig_bias[:], in0=as_cols[:, 0, :], in1=as_cols[:, 2, :])
            nc.vector.tensor_sub(out=u_diff[:], in0=as_cols[:, 1, :], in1=as_cols[:, 2, :])
            nc.scalar.activation(out=sig_pos[:], in_=u_diff[:], func=ACT.Sigmoid, scale=0.5)
            nc.scalar.activation(out=sig_neg[:], in_=u_diff[:], func=ACT.Sigmoid, scale=-0.5)

        def drip(steps, count=1):
            for step in steps[:count]:
                step()
            for step in steps[:count]:
                steps.remove(step)

        gain_steps = [
            lambda: nc.vector.reciprocal(out=inv_neg[:], in_=sig_neg[:]),
            lambda: nc.vector.reciprocal(out=inv_pos[:], in_=sig_pos[:]),
            lambda: nc.vector.tensor_mul(out=root[:], in0=sig_pos[:], in1=inv_neg[:]),
            lambda: nc.vector.tensor_mul(out=inv_root[:], in0=sig_neg[:], in1=inv_pos[:]),
            lambda: nc.vector.tensor_sub(out=gain[:], in0=root[:], in1=inv_root[:]),
            lambda: nc.vector.tensor_scalar(
                out=nudge[:], in0=gain[:], scalar1=0.0, scalar2=TINY, op0=ALU.is_equal, op1=ALU.mult
            ),
            lambda: nc.vector.tensor_add(out=factor[:], in0=gain[:], in1=nudge[:]),
            lambda: nc.vector.tensor_mul(out=rise[:], in0=factor[:], in1=root[:]),
            lambda: nc.vector.tensor_mul(out=factor_pairs[:], in0=factor[:, 0:2], in1=factor[:, 2:4]),
            lambda: nc.vector.reciprocal(out=shift[:], in_=rise[:]),
            lambda: nc.vector.tensor_mul(out=factor_all[:], in0=factor_pairs[:, 0:1], in1=factor_pairs[:, 1:2]),
            lambda: nc.vector.tensor_mul(out=factor_shift[:], in0=factor_all[:], in1=shift[:, 0:1]),
        ]
        spread = {}

        def spread_u_sum():
            spread[0] = flip_pool.tile([P, P], F32, name="bank")
            nc.tensor.transpose(spread[0][:], u_sum[:, 0:1].to_broadcast([P, P]), ident[:])

        offset_steps = [
            lambda: nc.vector.tensor_reduce(out=u_total[:], in_=spread[0][:], axis=mybir.AxisListType.X, op=ALU.add),
            lambda: nc.vector.tensor_sub(out=y_raw[:], in0=y_all[:, 0:1], in1=y_all[:, 1:2]),
            lambda: nc.vector.tensor_scalar(
                out=y_diff[:], in0=u_total[:], scalar1=0.5, scalar2=y_raw[:, 0:1], op0=ALU.mult, op1=ALU.add
            ),
            lambda: nc.vector.tensor_scalar(
                out=y_diff_neg[:], in0=y_diff[:], scalar1=-1.0, scalar2=0.0, op0=ALU.mult, op1=ALU.add
            ),
        ]

        sorted_x = {}
        grouped = {}
        codes = {}
        planes = {}
        on = {}
        running = {}
        product = const.tile([P, BATCH], F32, align_bytes=256)

        def words_of(n):
            words = x_pairs[n][:].rearrange("b j k -> b (j k)").bitcast(F32)
            return words.rearrange("b (s p u) -> b s u p", s=PAIR_TILES * PASSES, u=2)

        def sort_tile(n):
            sorted_x[n] = mx_pool.tile([P, PAIR_TILES * PASSES, 2, P], F32, name="sorted_x", align_bytes=256)

        def sort_in_quarters(n):
            sort_tile(n)
            for j, h in QUARTER_ORDER:
                part = slice(PASSES * j + 2 * h, PASSES * j + 2 * h + 2)
                nc.vector.tensor_copy(out=sorted_x[n][:, part], in_=words_of(n)[:, part])
                if n == 1:
                    drip(gain_steps)

        def sort_x(n):
            if n < PAIRS:
                sort_tile(n)
                nc.vector.tensor_copy(out=sorted_x[n][:], in_=words_of(n))

        banks = {}

        def flip_bank(n, i, loose=False):
            if i == 0:
                grouped[n] = mx_pool.tile([P, PASSES, 4 * PAIR], BF16, name="grouped", align_bytes=256)
            h, j = divmod(i, 2)
            bank = flip_pool.tile([P, 2, 2, P], F32, name="bank")
            banks[(n, i)] = bank
            for g in range(2):
                for u in range(2):
                    nc.tensor.transpose(bank[:, g, u, :], (words_of(n) if loose else sorted_x[n])[:, PASSES * j + 2 * h + g, u, :], ident[:])

        def empty_bank(n, i, vector):
            h, j = divmod(i, 2)
            dest = grouped[n][:].bitcast(F32).rearrange("p g (b u) -> p g b u", u=2)
            place = dest[:, 2 * h : 2 * h + 2, j * P : (j + 1) * P, :]
            if vector:
                nc.vector.tensor_copy(out=place, in_=banks[(n, i)][:].rearrange("p g u b -> p g b u"))
            else:
                nc.scalar.copy(out=place, in_=banks[(n, i)][:].rearrange("p g u b -> p g b u"))

        def transpose_x(n, loose=False):
            for i in range(4):
                flip_bank(n, i, loose)

        def empty_banks(n, engines="ssss"):
            for i in range(4):
                empty_bank(n, i, engines[i] == "v")

        def quantise(n, g0=0, g1=PASSES):
            if n < PAIRS:
                if g0 == 0:
                    codes[n] = mx_pool.tile([P, PASSES, PAIR], U32, name="codes", align_bytes=256)
                    planes[n] = mx_pool.tile([P, PASSES, PAIR], U8, name="planes", align_bytes=256)
                nc.vector.quantize_mx(
                    out=codes[n][:, g0:g1, :].rearrange("p g b -> p (g b)").bitcast(FP8X4),
                    scales=planes[n][:, g0:g1, :].rearrange("p g b -> p (g b)"),
                    in_=grouped[n][:, g0:g1, :].rearrange("p g w -> p (g w)"),
                )

        def multiply(n, between=None):
            c, second = divmod(n, 2)
            cols = slice(second * PAIR, (second + 1) * PAIR)
            alone = n == PAIRS - 1
            for t in range(HID_TILES):
                if not second:
                    on[(c, t)] = on_pool.tile([P, CHUNK], F32, name="on", align_bytes=256)
                side = 0 if alone else t % 2
                if alone:
                    acc = flip_pool.tile([P, 1, PAIR], F32, name="bank")
                elif side == 0:
                    acc = acc_pool.tile([P, 2, PAIR], F32, name="acc")
                hid = slice(t * P, (t + 1) * P)
                for g in range(PASSES):
                    nc.tensor.matmul_mx(
                        out=acc[:, side, :],
                        lhsT=w_codes[:, g, hid].bitcast(FP8X4),
                        lhsT_scale=w_planes[:, g, hid],
                        rhs=codes[n][:, g, :].bitcast(FP8X4),
                        rhs_scale=planes[n][:, g, :],
                        start=(g == 0),
                        stop=(g == PASSES - 1),
                    )
                if alone or side == 1:
                    for i in range(side + 1):
                        hidden = t - side + i
                        nc.scalar.activation(
                            out=on[(c, hidden)][:, cols], in_=acc[:, i, :], func=ACT.Sigmoid,
                            bias=sig_bias[:, hidden : hidden + 1],
                        )
                    if t == 1 and between:
                        between()

        def extend_product(c, t, cols=slice(0, CHUNK), scalar=False):
            if t < HID_TILES - 1:
                if (c, t) not in running:
                    running[(c, t)] = run_pool.tile([P, CHUNK], F32, name="run%d" % t, align_bytes=256)
                dest = running[(c, t)][:, cols]
            else:
                dest = product[:, c * CHUNK + cols.start : c * CHUNK + cols.stop]
            if t == 0 and scalar:
                nc.scalar.activation(
                    out=dest, in_=on[(c, 0)][:, cols], func=ACT.Identity, scale=factor_all[:, 0:1], bias=factor_shift[:, 0:1]
                )
            elif t == 0:
                nc.vector.tensor_scalar(
                    out=dest, in0=on[(c, 0)][:, cols], scalar1=shift[:, 0:1], scalar2=factor_all[:, 0:1],
                    op0=ALU.add, op1=ALU.mult,
                )
            else:
                nc.vector.scalar_tensor_tensor(
                    out=dest, in0=on[(c, t)][:, cols], scalar=shift[:, t : t + 1], in1=running[(c, t - 1)][:, cols],
                    op0=ALU.add, op1=ALU.mult,
                )

        sixteens = const.tile([P, BATCH_TILES, P // 4], F32, align_bytes=256)
        powers = const.tile([P, BATCH_TILES, P // 4], I32, align_bytes=256)
        scaled = const.tile([P, BATCH_TILES, P // 4], F32, align_bytes=256)
        mantissa = const.tile([P, BATCH_TILES], F32)
        fields = const.tile([P, BATCH_TILES], F32)
        back = {}

        def turn_back(first, count):
            back[first] = flip_pool.tile([P, count, P], F32, name="bank")
            for j in range(count):
                nc.tensor.transpose(back[first][:, j, :], product[:, (first + j) * P : (first + j + 1) * P], ident[:])

        def multiply_neighbours(first, count):
            nc.vector.tensor_reduce(
                out=sixteens[:, first : first + count, :],
                in_=back[first][:].rearrange("b j (q w) -> b j q w", w=4),
                axis=mybir.AxisListType.X, op=ALU.mult,
            )

        def find_powers(first, count):
            tiles = slice(first, first + count)
            nc.vector.tensor_scalar(
                out=powers[:, tiles, :], in0=sixteens[:, tiles, :].bitcast(I32), scalar1=EXPONENT_BITS, scalar2=EXPONENT_BITS,
                op0=ALU.bitwise_and, op1=ALU.bitwise_xor,
            )

        def scale_by_powers(first, count):
            tiles = slice(first, first + count)
            nc.vector.tensor_mul(out=scaled[:, tiles, :], in0=sixteens[:, tiles, :], in1=powers[:, tiles, :].bitcast(F32))

        def reduce_fields(first, count):
            tiles = slice(first, first + count)
            nc.vector.tensor_reduce(out=fields[:, tiles], in_=powers[:, tiles, :], axis=mybir.AxisListType.X, op=ALU.add)

        def reduce_mantissas(first, count):
            tiles = slice(first, first + count)
            nc.vector.tensor_reduce(out=mantissa[:, tiles], in_=scaled[:, tiles, :], axis=mybir.AxisListType.X, op=ALU.mult)

        logit_diff = const.tile([P, BATCH_TILES], F32)
        rest_logs = const.tile([P, BATCH_TILES], F32)
        power_logs = const.tile([P, BATCH_TILES], F32)
        logs = {}

        def log_rests(first, count):
            nc.scalar.activation(out=rest_logs[:, first : first + count], in_=mantissa[:, first : first + count], func=ACT.Ln, scale=2.0 ** -48)

        def log_powers(first, count):
            nc.vector.tensor_scalar(
                out=power_logs[:, first : first + count], in0=fields[:, first : first + count],
                scalar1=-(32 * 127 + 48) * FIELD, scalar2=-LN_2 / FIELD, op0=ALU.add, op1=ALU.mult,
            )

        def add_logs(first, count):
            tiles = slice(first, first + count)
            nc.vector.tensor_add(out=logit_diff[:, tiles], in0=rest_logs[:, tiles], in1=power_logs[:, tiles])

        def log_products(first, count):
            logs[first] = run_pool.tile([P, count, P], F32, name="logs%d" % count, align_bytes=256)
            nc.scalar.activation(out=logs[first][:], in_=back[first][:], func=ACT.Ln)

        twos = {}

        def multiply_pairs(first, count):
            twos[first] = run_pool.tile([P, count, P // 2], F32, name="twos", align_bytes=256)
            nc.vector.tensor_reduce(
                out=twos[first][:], in_=back[first][:].rearrange("b j (q w) -> b j q w", w=2),
                axis=mybir.AxisListType.X, op=ALU.mult,
            )

        def log_pairs(first, count):
            logs[first] = run_pool.tile([P, count, P // 2], F32, name="logs_of_twos", align_bytes=256)
            nc.scalar.activation(out=logs[first][:], in_=twos[first][:], func=ACT.Ln)

        def sum_logs(first, count):
            nc.vector.tensor_reduce(
                out=logit_diff[:, first : first + count], in_=logs[first][:], axis=mybir.AxisListType.X, op=ALU.add
            )

        constants_onto_partitions()
        transpose_x(0, loose=True)
        empty_bank(0, 0, False)
        empty_bank(0, 1, True)
        quantise(0, 0, 2)
        empty_bank(0, 2, False)
        empty_bank(0, 3, False)
        columns = constants_transposed()
        quantise(0, 2, 4)
        bias_and_difference(columns)
        sort_in_quarters(1)
        nc.vector.tensor_reduce(out=u_sum[:], in_=u_diff[:], axis=mybir.AxisListType.X, op=ALU.add)
        drip(gain_steps)
        multiply(0)
        transpose_x(1)
        empty_banks(1, "svsv")
        quantise(1, 0, 2)
        drip(gain_steps)
        quantise(1, 2, 4)
        drip(gain_steps, 2)
        transpose_x(2, loose=True)
        empty_banks(2)
        load_x(X_AHEAD)
        sort_x(3)
        drip(gain_steps)
        for n in range(1, PAIRS - 3):
            c, second = divmod(n, 2)
            done = c - 1
            load_x(n + X_AHEAD)
            step = 2 * second + min(done, 1)
            if done >= 0:
                extend_product(done, step)
            if n >= 5 and second:
                multiply_neighbours(4 * (c - 2), 4)
            if n in (8, 12):
                find_powers(2 * n - 16, 8)
            if n == 9:
                scale_by_powers(0, 8)
            if n == 10:
                reduce_mantissas(0, 8)
            quantise(n + 1)
            if n == 1:
                drip(gain_steps)
            if n > 2:
                drip(offset_steps)
            multiply(n, (lambda chunk=c: extend_product(chunk, 0, scalar=True)) if second and c > 0 else None)
            if done >= 0 and step + 1 < HID_TILES:
                extend_product(done, step + 1)
            if n == 10:
                reduce_fields(0, 8)
            if n < DEEPER:
                sort_x(n + 3)
            if n >= DEEPER - 1:
                sort_x(n + 4)
            if n == 1:
                drip(gain_steps)
            if n > 2:
                drip(offset_steps)
            for m in range(n + 2 if n <= DEEPER else n + 3, n + 3 if n < DEEPER else n + 4):
                transpose_x(m)
                empty_banks(m)
            if n == 1:
                drip(gain_steps)
            if n == 2:
                spread_u_sum()
            if n >= 4 and not second:
                turn_back(4 * (c - 2), 4)
        first, last = slice(0, PAIR), slice(PAIR, CHUNK)
        extend_product(5, 3)
        turn_back(20, 4)
        quantise(14)
        scale_by_powers(8, 8)
        reduce_fields(8, 8)
        multiply_neighbours(16, 4)
        multiply(13, lambda: extend_product(6, 0, slice(0, CHUNK), scalar=True))
        quantise(15)
        multiply_neighbours(20, 4)
        extend_product(6, 1)
        reduce_mantissas(8, 8)
        extend_product(6, 2)
        find_powers(16, 8)
        multiply(14, lambda: extend_product(7, 0, first, scalar=True))
        reduce_fields(16, 8)
        extend_product(6, 3)
        scale_by_powers(16, 8)
        multiply(15, lambda: extend_product(7, 0, last, scalar=True))
        turn_back(24, 4)
        extend_product(7, 1, first)
        reduce_mantissas(16, 8)
        extend_product(7, 2, first)
        extend_product(7, 1, last)
        extend_product(7, 3, first)
        turn_back(28, 2)
        extend_product(7, 2, last)
        log_powers(0, 24)
        extend_product(7, 3, last)
        turn_back(30, 2)
        multiply_pairs(24, 4)
        multiply_pairs(28, 2)
        log_rests(0, 24)
        log_products(30, 2)
        log_pairs(24, 4)
        log_pairs(28, 2)
        add_logs(0, 24)
        sum_logs(30, 2)
        sum_logs(24, 4)
        sum_logs(28, 2)

        probs = const.tile([P, BATCH_TILES, 2], F32)
        nc.scalar.activation(out=probs[:, :, 0], in_=logit_diff[:], func=ACT.Sigmoid, bias=y_diff[:, 0:1])
        nc.scalar.activation(
            out=probs[:, :, 1], in_=logit_diff[:], func=ACT.Sigmoid, bias=y_diff_neg[:, 0:1], scale=-1.0
        )
        nc.sync.dma_start(
            out=out.rearrange("(p i) c -> p (i c)", i=BATCH_TILES),
            in_=probs[:].rearrange("p i c -> p (i c)"),
        )
